import numpy as np
import ml_dtypes


def mxq(x, axis, fmt="e4m3"):
    dtype, down = {"e4m3": (ml_dtypes.float8_e4m3fn, 7), "e5m2": (ml_dtypes.float8_e5m2, 14)}[fmt]
    v = np.moveaxis(np.asarray(x, np.float32).astype(ml_dtypes.bfloat16).astype(np.float64), axis, -1)
    blocks = v.reshape(v.shape[:-1] + (-1, 32))
    amax = np.abs(blocks).max(-1, keepdims=True)
    byte = np.maximum(np.where(amax > 0, np.frexp(amax)[1] - 1 + 127, 0) - down, 1)
    scale = np.exp2(byte - 127.0)
    codes = (blocks / scale).astype(np.float32).astype(dtype).astype(np.float64)
    return np.moveaxis((codes * scale).reshape(v.shape), -1, axis)


WIDE = False


def mx_kscale(k):
    if not WIDE:
        return np.ones(k)
    levels = np.array([10, -10, 5, -5, 0])
    if k % 512:
        return np.exp2(np.random.permutation(np.resize(levels, k // 32))).repeat(32)
    a = np.empty((k // 512, 16))
    for p in range(k // 512):
        a[p, :8] = np.random.permutation(np.resize(levels, 8))
        for g in range(8):
            far = levels[np.abs(levels - a[p, g]) >= 10]
            a[p, g + 8] = far[np.random.randint(len(far))]
    return np.exp2(a.ravel()).repeat(32)


BF16 = ml_dtypes.bfloat16


def bf(x):
    return np.asarray(x, np.float32).astype(BF16)


def f64(x):
    return np.asarray(x).astype(np.float64)


B, L, D, O = 16, 256, 1024, 1


def setup_inputs():
    s, t = mx_kscale(D), mx_kscale(D)
    return {"input1": bf(np.random.standard_normal((B, L, D)) * s),
            "input2": bf(np.random.standard_normal((B, L, D)) / t),
            "w1": bf(np.random.standard_normal((D, O, D)) * (4.0 / D) / s[:, None, None] * t),
            "aff1": bf(np.random.standard_normal((B, L, O))),
            "aff2": bf(np.random.standard_normal((B, L, O))),
            "bias": bf(1.0 + 0.25 * np.random.standard_normal(O))}


def reference(input1, input2, w1, aff1, aff2, bias):
    u = mxq(f64(input1), 2, "e4m3").reshape(B * L, D) @ mxq(f64(w1), 0, "e4m3").reshape(D, O * D)
    u = u.reshape(B, L * O, D)
    p = mxq(u, 2, "e4m3") @ mxq(f64(input2), 2, "e4m3").transpose(0, 2, 1)
    logits_1 = p.reshape(B, L, O, L).transpose(0, 1, 3, 2)
    logits_2 = f64(aff1)[:, :, None, :] + f64(aff2)[:, None, :, :] + f64(bias)
    return logits_1 + logits_2

@@ -1,0 +1,230 @@
+from contextlib import ExitStack
+
+import concourse.mybir as mybir
+from concourse.masks import make_identity
+
+F32 = mybir.dt.float32
+BF16 = mybir.dt.bfloat16
+U32 = mybir.dt.uint32
+U8 = mybir.dt.uint8
+FP8X4 = mybir.dt.float8_e4m3fn_x4
+ADD = mybir.AluOpType.add
+
+B, L, D = 16, 256, 1024
+P = 128
+PACK = 4
+K_PASS = P * PACK
+PASSES = D // K_PASS
+ROW_TILES = L // P
+PAIR = 2
+HALVES = PACK // PAIR
+AHEAD = 4
+
+FLOPS = 2 * B * L * D * D + 2 * B * L * L * D
+
+
+def tile_biaffine_2_pa_t_kernel(tc, input1, input2, w1, aff1, aff2, bias, out):
+    nc = tc.nc
+    with ExitStack() as ctx:
+        const = ctx.enter_context(tc.tile_pool(name="const", bufs=1))
+        w_stage = ctx.enter_context(tc.tile_pool(name="w_stage", bufs=2))
+        raw_pool = ctx.enter_context(tc.tile_pool(name="raw", bufs=AHEAD + 1))
+        grouped_pool = ctx.enter_context(tc.tile_pool(name="grouped", bufs=3))
+        codes_pool = ctx.enter_context(tc.tile_pool(name="codes", bufs=3))
+        result_pool = ctx.enter_context(tc.tile_pool(name="result", bufs=3))
+        psum_t = ctx.enter_context(tc.psum_pool(name="psum_t", bufs=4))
+        psum_u = ctx.enter_context(tc.psum_pool(name="psum_u", bufs=3))
+        psum_o = ctx.enter_context(tc.psum_pool(name="psum_o", bufs=1))
+        ctx.enter_context(tc.manual_schedule())
+
+        def bank_copy(index):
+            return nc.vector.tensor_copy if index % 4 == 3 else nc.scalar.copy
+
+        def load_tokens(tokens, name):
+            raw = raw_pool.tile([P, ROW_TILES, D], BF16, name=name, tag=name)
+            nc.sync.dma_start(out=raw[:], in_=tokens.rearrange("(q r) k -> q r k", r=ROW_TILES))
+            return raw
+
+        in1_raw = {}
+        in2_raw = {}
+
+        def load_round(n):
+            if n + 1 < B:
+                in1_raw[n + 1] = load_tokens(input1[n + 1], "in1_raw")
+            if n < B:
+                in2_raw[n] = load_tokens(input2[n], "in2_raw")
+
+        def load_w_half(g2):
+            w_raw = w_stage.tile([P, PASSES * PACK, K_PASS], BF16, name="w_raw", tag="w_raw")
+            for g1 in range(PASSES):
+                nc.sync.dma_start(
+                    out=w_raw[:, PACK * g1 : PACK * (g1 + 1), :],
+                    in_=w1[K_PASS * g1 : K_PASS * (g1 + 1), 0, K_PASS * g2 : K_PASS * (g2 + 1)].rearrange(
+                        "(q t) j -> q t j", t=PACK
+                    ),
+                )
+            return w_raw
+
+        def transpose_tokens(raw):
+            words = raw[:].bitcast(F32)
+            banks = []
+            for g in range(PASSES):
+                t_bank = psum_t.tile([P, ROW_TILES, HALVES, P], F32, name="t_bank", tag="t_bank")
+                for r in range(ROW_TILES):
+                    for u in range(HALVES):
+                        first = g * HALVES * P + u
+                        last = (g + 1) * HALVES * P
+                        nc.tensor.transpose(t_bank[:, r, u, :], words[:, r, first:last:HALVES], ident_f32[:])
+                banks.append(t_bank)
+            return banks
+
+        def group_tokens(banks, first_index, name):
+            grouped = grouped_pool.tile([P, PASSES, L * PACK], BF16, name=name, tag=name, align_bytes=64)
+            grouped_words = grouped[:].bitcast(F32)
+            for g in range(PASSES):
+                bank_copy(first_index + g)(
+                    out=grouped_words[:, g, :].rearrange("p (q r u) -> p q r u", r=ROW_TILES, u=HALVES),
+                    in_=banks[g][:].rearrange("p r u q -> p q r u"),
+                )
+            return grouped
+
+        def quantise(grouped_flat, name):
+            codes = codes_pool.tile([P, PASSES, L], U32, name=name + "_codes", tag=name + "_codes", align_bytes=64)
+            scales = codes_pool.tile([P, PASSES, L], U8, name=name + "_scales", tag=name + "_scales", align_bytes=64)
+            nc.vector.quantize_mx(
+                out=codes[:].rearrange("p g c -> p (g c)").bitcast(FP8X4),
+                scales=scales[:].rearrange("p g c -> p (g c)"),
+                in_=grouped_flat,
+            )
+            return codes, scales
+
+        def stage_one(in1_mx):
+            in1_codes, in1_scales = in1_mx
+            u_grouped = grouped_pool.tile([P, PASSES, L, PACK], BF16, name="u_grouped", tag="u_grouped", align_bytes=64)
+            for g2 in range(PASSES):
+                for m in range(ROW_TILES):
+                    x_cols = slice(m * P, (m + 1) * P)
+                    u_bank = psum_u.tile([P, PACK, P], F32, name="u_bank", tag="u_bank")
+                    for t2 in range(PACK):
+                        for g1 in range(PASSES):
+                            nc.tensor.matmul_mx(
+                                out=u_bank[:, t2, :],
+                                lhsT=w_codes[:, g2, t2, g1, :].bitcast(FP8X4),
+                                lhsT_scale=w_scales[:, g2, t2, g1, :],
+                                rhs=in1_codes[:, g1, x_cols].bitcast(FP8X4),
+                                rhs_scale=in1_scales[:, g1, x_cols],
+                                start=(g1 == 0),
+                                stop=(g1 == PASSES - 1),
+                            )
+                    bank_copy(g2 * ROW_TILES + m)(
+                        out=u_grouped[:, g2, x_cols, :], in_=u_bank[:].rearrange("p t x -> p x t")
+                    )
+            return u_grouped
+
+        def stage_two(u_mx, in2_mx):
+            u_codes, u_scales = u_mx
+            in2_codes, in2_scales = in2_mx
+            o_bank = psum_o.tile([P, ROW_TILES, L], F32, name="o_bank", tag="o_bank")
+            for m in range(ROW_TILES):
+                x_cols = slice(m * P, (m + 1) * P)
+                for g2 in range(PASSES):
+                    nc.tensor.matmul_mx(
+                        out=o_bank[:, m, :],
+                        lhsT=u_codes[:, g2, x_cols].bitcast(FP8X4),
+                        lhsT_scale=u_scales[:, g2, x_cols],
+                        rhs=in2_codes[:, g2, :].bitcast(FP8X4),
+                        rhs_scale=in2_scales[:, g2, :],
+                        start=(g2 == 0),
+                        stop=(g2 == PASSES - 1),
+                    )
+            return o_bank
+
+        def finish(b, o_bank):
+            result = result_pool.tile([P, ROW_TILES, L], F32, name="result", tag="result")
+            for m in range(ROW_TILES):
+                nc.vector.scalar_tensor_tensor(
+                    out=result[:, m, :],
+                    in0=o_bank[:, m, :],
+                    scalar=aff1_col[:, b * ROW_TILES + m : b * ROW_TILES + m + 1],
+                    in1=aff2_all[:, b * L : (b + 1) * L],
+                    op0=ADD,
+                    op1=ADD,
+                )
+            nc.sync.dma_start(out=out[b].rearrange("(m p) y o -> p m (y o)", p=P), in_=result[:])
+
+        ident_f32 = const.tile([P, P], F32, name="ident_f32")
+        make_identity(nc, ident_f32[:])
+        ident_bf16 = const.tile([P, P], BF16, name="ident_bf16")
+        make_identity(nc, ident_bf16[:])
+
+        aff_rows = const.tile([P, P], BF16, name="aff_rows")
+        nc.vector.memset(aff_rows[:], 0.0)
+        nc.sync.dma_start(
+            out=aff_rows[0 : B * ROW_TILES, :], in_=aff1.rearrange("b (m p) o -> (b m) (p o)", p=P)
+        )
+        bias_bf16 = const.tile([P, 1], BF16, name="bias_bf16")
+        nc.sync.dma_start(out=bias_bf16[:], in_=bias.partition_broadcast(P))
+
+        in1_raw[0] = load_tokens(input1[0], "in1_raw")
+        w_raw_halves = [load_w_half(g2) for g2 in range(PASSES)]
+        load_round(0)
+        aff2_all = const.tile([P, B * L], BF16, name="aff2_all")
+        nc.sync.dma_start(out=aff2_all[:], in_=aff2.rearrange("b y o -> (b y o)").partition_broadcast(P))
+        for n in range(1, AHEAD):
+            load_round(n)
+
+        aff_bank = psum_o.tile([P, P], BF16, name="aff_bank", tag="o_bank")
+        nc.tensor.transpose(aff_bank[:], aff_rows[:], ident_bf16[:])
+        bias_f32 = const.tile([P, 1], F32, name="bias_f32")
+        nc.vector.tensor_copy(out=bias_f32[:], in_=bias_bf16[:])
+        aff1_col = const.tile([P, B * ROW_TILES], F32, name="aff1_col")
+        nc.vector.tensor_scalar(
+            out=aff1_col[:], in0=aff_bank[:, 0 : B * ROW_TILES], scalar1=bias_f32[:, 0:1], scalar2=None, op0=ADD
+        )
+
+        in1_mx = {}
+        in2_mx = {}
+        u_grouped = {}
+        u_mx = {}
+        o_banks = {}
+
+        in1_grouped = group_tokens(transpose_tokens(in1_raw[0]), 2, "in1_grouped")
+        in1_mx[0] = quantise(in1_grouped[:].rearrange("p g c -> p (g c)"), "in1")
+
+        w_codes = const.tile([P, PASSES, PACK, PASSES, P], U32, name="w_codes", align_bytes=64)
+        w_scales = const.tile([P, PASSES, PACK, PASSES, P], U8, name="w_scales", align_bytes=64)
+        for g2 in range(PASSES):
+            w_grouped = w_stage.tile([P, PACK, PASSES, P, PACK], BF16, name="w_grouped", tag="w_grouped", align_bytes=64)
+            w_sorted = w_raw_halves[g2][:].rearrange(
+                "p (g t) (q s) -> p s g q t", g=PASSES, s=PACK
+            )
+            for t2 in range(PACK):
+                copy = nc.vector.tensor_copy if t2 % 2 == 0 else nc.scalar.copy
+                copy(out=w_grouped[:, t2], in_=w_sorted[:, t2])
+            for t2 in range(PACK):
+                nc.vector.quantize_mx(
+                    out=w_codes[:, g2, t2].rearrange("p g q -> p (g q)").bitcast(FP8X4),
+                    scales=w_scales[:, g2, t2].rearrange("p g q -> p (g q)"),
+                    in_=w_grouped[:, t2].rearrange("p g q t -> p (g q t)"),
+                )
+
+        for n in range(B + 2):
+            if 1 <= n <= B:
+                u_mx[n - 1] = quantise(u_grouped[n - 1][:].rearrange("p g x t -> p (g x t)"), "u")
+            if n >= 2:
+                finish(n - 2, o_banks[n - 2])
+            load_round(n + AHEAD)
+            if n < B:
+                banks = []
+                if n + 1 < B:
+                    banks = transpose_tokens(in1_raw[n + 1])
+                banks = banks + transpose_tokens(in2_raw[n])
+                if n + 1 < B:
+                    in1_grouped = group_tokens(banks[0:PASSES], 0, "in1_grouped")
+                in2_grouped = group_tokens(banks[-PASSES:], 2, "in2_grouped")
+                if n + 1 < B:
+                    in1_mx[n + 1] = quantise(in1_grouped[:].rearrange("p g c -> p (g c)"), "in1")
+                in2_mx[n] = quantise(in2_grouped[:].rearrange("p g c -> p (g c)"), "in2")
+                u_grouped[n] = stage_one(in1_mx[n])
+            if 1 <= n <= B:
+                o_banks[n - 1] = stage_two(u_mx[n - 1], in2_mx[n - 1])

@@ -29,6 +29,7 @@ def tile_biaffine_2_pa_t_kernel(tc, input1, input2, w1, aff1, aff2, bias, out):
         const = ctx.enter_context(tc.tile_pool(name="const", bufs=1))
         w_stage = ctx.enter_context(tc.tile_pool(name="w_stage", bufs=2))
         raw_pool = ctx.enter_context(tc.tile_pool(name="raw", bufs=AHEAD + 1))
+        ordered_pool = ctx.enter_context(tc.tile_pool(name="ordered", bufs=2))
         grouped_pool = ctx.enter_context(tc.tile_pool(name="grouped", bufs=3))
         codes_pool = ctx.enter_context(tc.tile_pool(name="codes", bufs=3))
         result_pool = ctx.enter_context(tc.tile_pool(name="result", bufs=3))
@@ -38,7 +39,7 @@ def tile_biaffine_2_pa_t_kernel(tc, input1, input2, w1, aff1, aff2, bias, out):
         ctx.enter_context(tc.manual_schedule())
 
         def bank_copy(index):
-            return nc.vector.tensor_copy if index % 4 == 3 else nc.scalar.copy
+            return nc.vector.tensor_copy if index == 3 else nc.scalar.copy
 
         def load_tokens(tokens, name):
             raw = raw_pool.tile([P, ROW_TILES, D], BF16, name=name, tag=name)
@@ -64,6 +65,24 @@ def tile_biaffine_2_pa_t_kernel(tc, input1, input2, w1, aff1, aff2, bias, out):
                     ),
                 )
             return w_raw
+
+        def order_tokens(raw, name):
+            ordered = ordered_pool.tile([P, ROW_TILES, PASSES, HALVES, P], F32, name=name, tag=name)
+            nc.vector.tensor_copy(
+                out=ordered[:],
+                in_=raw[:].bitcast(F32).rearrange("q r (g p u) -> q r g u p", g=PASSES, u=HALVES),
+            )
+            return ordered
+
+        def transpose_ordered(ordered):
+            banks = []
+            for g in range(PASSES):
+                t_bank = psum_t.tile([P, ROW_TILES, HALVES, P], F32, name="t_bank", tag="t_bank")
+                for r in range(ROW_TILES):
+                    for u in range(HALVES):
+                        nc.tensor.transpose(t_bank[:, r, u, :], ordered[:, r, g, u, :], ident_f32[:])
+                banks.append(t_bank)
+            return banks
 
         def transpose_tokens(raw):
             words = raw[:].bitcast(F32)
@@ -116,7 +135,7 @@ def tile_biaffine_2_pa_t_kernel(tc, input1, input2, w1, aff1, aff2, bias, out):
                                 start=(g1 == 0),
                                 stop=(g1 == PASSES - 1),
                             )
-                    bank_copy(g2 * ROW_TILES + m)(
+                    nc.scalar.copy(
                         out=u_grouped[:, g2, x_cols, :], in_=u_bank[:].rearrange("p t x -> p x t")
                     )
             return u_grouped
@@ -208,17 +227,23 @@ def tile_biaffine_2_pa_t_kernel(tc, input1, input2, w1, aff1, aff2, bias, out):
                     in_=w_grouped[:, t2].rearrange("p g q t -> p (g q t)"),
                 )
 
+        in1_ordered = {}
+        in2_ordered = {}
         for n in range(B + 2):
+            if n + 2 < B:
+                in1_ordered[n + 2] = order_tokens(in1_raw[n + 2], "in1_ordered")
             if 1 <= n <= B:
                 u_mx[n - 1] = quantise(u_grouped[n - 1][:].rearrange("p g x t -> p (g x t)"), "u")
+            if n + 1 < B:
+                in2_ordered[n + 1] = order_tokens(in2_raw[n + 1], "in2_ordered")
             if n >= 2:
                 finish(n - 2, o_banks[n - 2])
             load_round(n + AHEAD)
             if n < B:
                 banks = []
                 if n + 1 < B:
-                    banks = transpose_tokens(in1_raw[n + 1])
-                banks = banks + transpose_tokens(in2_raw[n])
+                    banks = transpose_ordered(in1_ordered[n + 1]) if n > 0 else transpose_tokens(in1_raw[n + 1])
+                banks = banks + (transpose_ordered(in2_ordered[n]) if n > 0 else transpose_tokens(in2_raw[n]))
                 if n + 1 < B:
                     in1_grouped = group_tokens(banks[0:PASSES], 0, "in1_grouped")
                 in2_grouped = group_tokens(banks[-PASSES:], 2, "in2_grouped")

@@ -17,6 +17,7 @@ K_PASS = P * PACK
 PASSES = D // K_PASS
 ROW_TILES = L // P
 PAIR = 2
+RUN = 16
 HALVES = PACK // PAIR
 AHEAD = 4
 
@@ -27,8 +28,8 @@ def tile_biaffine_2_pa_t_kernel(tc, input1, input2, w1, aff1, aff2, bias, out):
     nc = tc.nc
     with ExitStack() as ctx:
         const = ctx.enter_context(tc.tile_pool(name="const", bufs=1))
-        w_stage = ctx.enter_context(tc.tile_pool(name="w_stage", bufs=2))
-        raw_pool = ctx.enter_context(tc.tile_pool(name="raw", bufs=AHEAD + 1))
+        w_stage = ctx.enter_context(tc.tile_pool(name="w_stage", bufs=PASSES * PASSES))
+        raw_pool = ctx.enter_context(tc.tile_pool(name="raw", bufs=AHEAD + 2))
         ordered_pool = ctx.enter_context(tc.tile_pool(name="ordered", bufs=2))
         grouped_pool = ctx.enter_context(tc.tile_pool(name="grouped", bufs=3))
         codes_pool = ctx.enter_context(tc.tile_pool(name="codes", bufs=3))
@@ -49,28 +50,37 @@ def tile_biaffine_2_pa_t_kernel(tc, input1, input2, w1, aff1, aff2, bias, out):
         in1_raw = {}
         in2_raw = {}
 
-        def load_round(n):
-            if n + 1 < B:
-                in1_raw[n + 1] = load_tokens(input1[n + 1], "in1_raw")
-            if n < B:
-                in2_raw[n] = load_tokens(input2[n], "in2_raw")
+        def load_in1(k):
+            if k < B:
+                in1_raw[k] = load_tokens(input1[k], "in1_raw")
 
-        def load_w_half(g2):
-            w_raw = w_stage.tile([P, PASSES * PACK, K_PASS], BF16, name="w_raw", tag="w_raw")
-            for g1 in range(PASSES):
-                nc.sync.dma_start(
-                    out=w_raw[:, PACK * g1 : PACK * (g1 + 1), :],
-                    in_=w1[K_PASS * g1 : K_PASS * (g1 + 1), 0, K_PASS * g2 : K_PASS * (g2 + 1)].rearrange(
-                        "(q t) j -> q t j", t=PACK
-                    ),
-                )
+        def load_in2(k):
+            if k < B:
+                in2_raw[k] = load_tokens(input2[k], "in2_raw")
+
+        def load_w_block(g2, g1):
+            w_raw = w_stage.tile([P, PACK, K_PASS], BF16, name="w_raw", tag="w_raw")
+            nc.sync.dma_start(
+                out=w_raw[:],
+                in_=w1[K_PASS * g1 : K_PASS * (g1 + 1), 0, K_PASS * g2 : K_PASS * (g2 + 1)].rearrange(
+                    "(q t) j -> q t j", t=PACK
+                ),
+            )
             return w_raw
 
-        def order_tokens(raw, name):
-            ordered = ordered_pool.tile([P, ROW_TILES, PASSES, HALVES, P], F32, name=name, tag=name)
+        def order_in1(raw):
+            ordered = ordered_pool.tile([P, ROW_TILES, PASSES, HALVES, P], F32, name="in1_ordered", tag="in1_ordered")
             nc.vector.tensor_copy(
                 out=ordered[:],
                 in_=raw[:].bitcast(F32).rearrange("q r (g p u) -> q r g u p", g=PASSES, u=HALVES),
+            )
+            return ordered
+
+        def order_in2(raw):
+            ordered = ordered_pool.tile([P, ROW_TILES, PASSES, HALVES, P], F32, name="in2_ordered", tag="in2_ordered")
+            nc.vector.tensor_copy(
+                out=ordered[:].bitcast(BF16).rearrange("q r g u (d i) -> q (r g) u d i", i=RUN),
+                in_=raw[:].rearrange("q r (g d u i) -> q (r g) u d i", g=PASSES, u=HALVES, i=RUN),
             )
             return ordered
 
@@ -117,58 +127,71 @@ def tile_biaffine_2_pa_t_kernel(tc, input1, input2, w1, aff1, aff2, bias, out):
             )
             return codes, scales
 
-        def stage_one(in1_mx):
-            in1_codes, in1_scales = in1_mx
-            u_grouped = grouped_pool.tile([P, PASSES, L, PACK], BF16, name="u_grouped", tag="u_grouped", align_bytes=64)
-            for g2 in range(PASSES):
-                for m in range(ROW_TILES):
-                    x_cols = slice(m * P, (m + 1) * P)
-                    u_bank = psum_u.tile([P, PACK, P], F32, name="u_bank", tag="u_bank")
-                    for t2 in range(PACK):
-                        for g1 in range(PASSES):
-                            nc.tensor.matmul_mx(
-                                out=u_bank[:, t2, :],
-                                lhsT=w_codes[:, g2, t2, g1, :].bitcast(FP8X4),
-                                lhsT_scale=w_scales[:, g2, t2, g1, :],
-                                rhs=in1_codes[:, g1, x_cols].bitcast(FP8X4),
-                                rhs_scale=in1_scales[:, g1, x_cols],
-                                start=(g1 == 0),
-                                stop=(g1 == PASSES - 1),
-                            )
-                    nc.scalar.copy(
-                        out=u_grouped[:, g2, x_cols, :], in_=u_bank[:].rearrange("p t x -> p x t")
-                    )
-            return u_grouped
+        def new_u_grouped():
+            return grouped_pool.tile(
+                [P, ROW_TILES, PASSES, P, PACK], BF16, name="u_grouped", tag="u_grouped", align_bytes=64
+            )
 
-        def stage_two(u_mx, in2_mx):
+        def stage_one(u_grouped, in1_mx, order):
+            in1_codes, in1_scales = in1_mx
+            for m, g2 in order:
+                x_cols = slice(m * P, (m + 1) * P)
+                u_bank = psum_u.tile([P, PACK, P], F32, name="u_bank", tag="u_bank")
+                for t2 in range(PACK):
+                    for g1 in range(PASSES):
+                        nc.tensor.matmul_mx(
+                            out=u_bank[:, t2, :],
+                            lhsT=w_codes[:, g2, t2, g1, :].bitcast(FP8X4),
+                            lhsT_scale=w_scales[:, g2, t2, g1, :],
+                            rhs=in1_codes[:, g1, x_cols].bitcast(FP8X4),
+                            rhs_scale=in1_scales[:, g1, x_cols],
+                            start=(g1 == 0),
+                            stop=(g1 == PASSES - 1),
+                        )
+                nc.scalar.copy(out=u_grouped[:, m, g2], in_=u_bank[:].rearrange("p t x -> p x t"))
+
+        def new_u_mx():
+            codes = codes_pool.tile([P, ROW_TILES, PASSES, P], U32, name="u_codes", tag="u_codes", align_bytes=64)
+            scales = codes_pool.tile([P, ROW_TILES, PASSES, P], U8, name="u_scales", tag="u_scales", align_bytes=64)
+            return codes, scales
+
+        def quantise_u(u_mx, u_grouped, m_part):
+            codes, scales = u_mx
+            nc.vector.quantize_mx(
+                out=codes[:, m_part].rearrange("p m g x -> p (m g x)").bitcast(FP8X4),
+                scales=scales[:, m_part].rearrange("p m g x -> p (m g x)"),
+                in_=u_grouped[:, m_part].rearrange("p m g x t -> p (m g x t)"),
+            )
+
+        def stage_two(o_parts, u_mx, in2_mx):
             u_codes, u_scales = u_mx
             in2_codes, in2_scales = in2_mx
-            o_bank = psum_o.tile([P, ROW_TILES, L], F32, name="o_bank", tag="o_bank")
             for m in range(ROW_TILES):
-                x_cols = slice(m * P, (m + 1) * P)
                 for g2 in range(PASSES):
                     nc.tensor.matmul_mx(
-                        out=o_bank[:, m, :],
-                        lhsT=u_codes[:, g2, x_cols].bitcast(FP8X4),
-                        lhsT_scale=u_scales[:, g2, x_cols],
+                        out=o_parts[m],
+                        lhsT=u_codes[:, m, g2, :].bitcast(FP8X4),
+                        lhsT_scale=u_scales[:, m, g2, :],
                         rhs=in2_codes[:, g2, :].bitcast(FP8X4),
                         rhs_scale=in2_scales[:, g2, :],
                         start=(g2 == 0),
                         stop=(g2 == PASSES - 1),
                     )
-            return o_bank
 
-        def finish(b, o_bank):
+        def add_affine(result_part, b, m, o_part):
+            nc.vector.scalar_tensor_tensor(
+                out=result_part,
+                in0=o_part,
+                scalar=aff1_col[:, b * ROW_TILES + m : b * ROW_TILES + m + 1],
+                in1=aff2_all[:, b * L : (b + 1) * L],
+                op0=ADD,
+                op1=ADD,
+            )
+
+        def finish(b, o_parts):
             result = result_pool.tile([P, ROW_TILES, L], F32, name="result", tag="result")
             for m in range(ROW_TILES):
-                nc.vector.scalar_tensor_tensor(
-                    out=result[:, m, :],
-                    in0=o_bank[:, m, :],
-                    scalar=aff1_col[:, b * ROW_TILES + m : b * ROW_TILES + m + 1],
-                    in1=aff2_all[:, b * L : (b + 1) * L],
-                    op0=ADD,
-                    op1=ADD,
-                )
+                add_affine(result[:, m, :], b, m, o_parts[m])
             nc.sync.dma_start(out=out[b].rearrange("(m p) y o -> p m (y o)", p=P), in_=result[:])
 
         ident_f32 = const.tile([P, P], F32, name="ident_f32")
@@ -184,13 +207,16 @@ def tile_biaffine_2_pa_t_kernel(tc, input1, input2, w1, aff1, aff2, bias, out):
         bias_bf16 = const.tile([P, 1], BF16, name="bias_bf16")
         nc.sync.dma_start(out=bias_bf16[:], in_=bias.partition_broadcast(P))
 
+        w_raw = {(0, g1): load_w_block(0, g1) for g1 in range(PASSES)}
         in1_raw[0] = load_tokens(input1[0], "in1_raw")
-        w_raw_halves = [load_w_half(g2) for g2 in range(PASSES)]
-        load_round(0)
         aff2_all = const.tile([P, B * L], BF16, name="aff2_all")
-        nc.sync.dma_start(out=aff2_all[:], in_=aff2.rearrange("b y o -> (b y o)").partition_broadcast(P))
-        for n in range(1, AHEAD):
-            load_round(n)
+        w_raw.update({(1, g1): load_w_block(1, g1) for g1 in range(PASSES)})
+        in1_raw[1] = load_tokens(input1[1], "in1_raw")
+        for n in range(AHEAD):
+            load_in1(n + 2)
+            load_in2(n)
+            if n == 1:
+                nc.sync.dma_start(out=aff2_all[:], in_=aff2.rearrange("b y o -> (b y o)").partition_broadcast(P))
 
         aff_bank = psum_o.tile([P, P], BF16, name="aff_bank", tag="o_bank")
         nc.tensor.transpose(aff_bank[:], aff_rows[:], ident_bf16[:])
@@ -205,51 +231,93 @@ def tile_biaffine_2_pa_t_kernel(tc, input1, input2, w1, aff1, aff2, bias, out):
         in2_mx = {}
         u_grouped = {}
         u_mx = {}
-        o_banks = {}
-
-        in1_grouped = group_tokens(transpose_tokens(in1_raw[0]), 2, "in1_grouped")
-        in1_mx[0] = quantise(in1_grouped[:].rearrange("p g c -> p (g c)"), "in1")
+        o_parts = {}
 
         w_codes = const.tile([P, PASSES, PACK, PASSES, P], U32, name="w_codes", align_bytes=64)
         w_scales = const.tile([P, PASSES, PACK, PASSES, P], U8, name="w_scales", align_bytes=64)
-        for g2 in range(PASSES):
+
+        def group_w(g2):
             w_grouped = w_stage.tile([P, PACK, PASSES, P, PACK], BF16, name="w_grouped", tag="w_grouped", align_bytes=64)
-            w_sorted = w_raw_halves[g2][:].rearrange(
-                "p (g t) (q s) -> p s g q t", g=PASSES, s=PACK
-            )
-            for t2 in range(PACK):
-                copy = nc.vector.tensor_copy if t2 % 2 == 0 else nc.scalar.copy
-                copy(out=w_grouped[:, t2], in_=w_sorted[:, t2])
-            for t2 in range(PACK):
+            for g1 in range(PASSES):
+                w_sorted = w_raw[g2, g1][:].rearrange(
+                    "p t (d u i e) -> p u e d i t", u=HALVES, i=RUN // PAIR, e=PAIR
+                )
+                for t2 in range(PACK):
+                    copy = nc.scalar.copy if t2 == 1 or (t2, g1) == (3, 0) else nc.vector.tensor_copy
+                    copy(
+                        out=w_grouped[:, t2, g1].rearrange("p (d i) t -> p d i t", i=RUN // PAIR),
+                        in_=w_sorted[:, t2 // PAIR, t2 % PAIR],
+                    )
+            return w_grouped
+
+        def quantise_w(g2, w_grouped):
+            for first in range(0, PACK, PAIR):
+                t2_pair = slice(first, first + PAIR)
                 nc.vector.quantize_mx(
-                    out=w_codes[:, g2, t2].rearrange("p g q -> p (g q)").bitcast(FP8X4),
-                    scales=w_scales[:, g2, t2].rearrange("p g q -> p (g q)"),
-                    in_=w_grouped[:, t2].rearrange("p g q t -> p (g q t)"),
+                    out=w_codes[:, g2, t2_pair].rearrange("p s g q -> p (s g q)").bitcast(FP8X4),
+                    scales=w_scales[:, g2, t2_pair].rearrange("p s g q -> p (s g q)"),
+                    in_=w_grouped[:, t2_pair].rearrange("p s g q t -> p (s g q t)"),
                 )
 
-        in1_ordered = {}
-        in2_ordered = {}
-        for n in range(B + 2):
+        w_grouped = group_w(0)
+        in1_grouped = group_tokens(transpose_tokens(in1_raw[0]), 0, "in1_grouped")
+        quantise_w(0, w_grouped)
+        w_grouped = group_w(1)
+        in1_mx[0] = quantise(in1_grouped[:].rearrange("p g c -> p (g c)"), "in1")
+        quantise_w(1, w_grouped)
+
+        in1_grouped = group_tokens(transpose_tokens(in1_raw[1]), 0, "in1_grouped")
+        in2_ordered = {0: order_in2(in2_raw[0])}
+        in1_mx[1] = quantise(in1_grouped[:].rearrange("p g c -> p (g c)"), "in1")
+        in1_ordered = {2: order_in1(in1_raw[2])}
+        load_in1(AHEAD + 2)
+        load_in2(AHEAD)
+        u_grouped[0] = new_u_grouped()
+        stage_one(u_grouped[0], in1_mx[0], [(m, g2) for g2 in range(PASSES) for m in range(ROW_TILES)])
+        in2_grouped = group_tokens(transpose_ordered(in2_ordered[0]), 2, "in2_grouped")
+        in2_ordered[1] = order_in2(in2_raw[1])
+        in2_mx[0] = quantise(in2_grouped[:].rearrange("p g c -> p (g c)"), "in2")
+
+        def by_row_tile(m_range):
+            return [(m, g2) for m in m_range for g2 in range(PASSES)]
+
+        all_m = range(ROW_TILES)
+        last = B - 1
+        for n in range(1, B):
             if n + 2 < B:
-                in1_ordered[n + 2] = order_tokens(in1_raw[n + 2], "in1_ordered")
-            if 1 <= n <= B:
-                u_mx[n - 1] = quantise(u_grouped[n - 1][:].rearrange("p g x t -> p (g x t)"), "u")
+                in1_ordered[n + 2] = order_in1(in1_raw[n + 2])
+            u_mx[n - 1] = new_u_mx()
+            quantise_u(u_mx[n - 1], u_grouped[n - 1], slice(0, ROW_TILES))
             if n + 1 < B:
-                in2_ordered[n + 1] = order_tokens(in2_raw[n + 1], "in2_ordered")
+                in2_ordered[n + 1] = order_in2(in2_raw[n + 1])
             if n >= 2:
-                finish(n - 2, o_banks[n - 2])
-            load_round(n + AHEAD)
-            if n < B:
-                banks = []
-                if n + 1 < B:
-                    banks = transpose_ordered(in1_ordered[n + 1]) if n > 0 else transpose_tokens(in1_raw[n + 1])
-                banks = banks + (transpose_ordered(in2_ordered[n]) if n > 0 else transpose_tokens(in2_raw[n]))
-                if n + 1 < B:
-                    in1_grouped = group_tokens(banks[0:PASSES], 0, "in1_grouped")
-                in2_grouped = group_tokens(banks[-PASSES:], 2, "in2_grouped")
-                if n + 1 < B:
-                    in1_mx[n + 1] = quantise(in1_grouped[:].rearrange("p g c -> p (g c)"), "in1")
-                in2_mx[n] = quantise(in2_grouped[:].rearrange("p g c -> p (g c)"), "in2")
-                u_grouped[n] = stage_one(in1_mx[n])
-            if 1 <= n <= B:
-                o_banks[n - 1] = stage_two(u_mx[n - 1], in2_mx[n - 1])
+                finish(n - 2, o_parts[n - 2])
+            load_in1(n + AHEAD + 2)
+            load_in2(n + AHEAD)
+            banks = []
+            if n < last:
+                banks = transpose_ordered(in1_ordered[n + 1])
+            banks = banks + transpose_ordered(in2_ordered[n])
+            if n < last:
+                in1_grouped = group_tokens(banks[0:PASSES], 0, "in1_grouped")
+            in2_grouped = group_tokens(banks[-PASSES:], 2, "in2_grouped")
+            if n < last:
+                in1_mx[n + 1] = quantise(in1_grouped[:].rearrange("p g c -> p (g c)"), "in1")
+            in2_mx[n] = quantise(in2_grouped[:].rearrange("p g c -> p (g c)"), "in2")
+            u_grouped[n] = new_u_grouped()
+            stage_one(u_grouped[n], in1_mx[n], by_row_tile(all_m if n < last else all_m[:1]))
+            o_bank = psum_o.tile([P, ROW_TILES, L], F32, name="o_bank", tag="o_bank")
+            o_parts[n - 1] = [o_bank[:, m, :] for m in all_m]
+            stage_two(o_parts[n - 1], u_mx[n - 1], in2_mx[n - 1])
+
+        stage_one(u_grouped[last], in1_mx[last], by_row_tile(all_m[1:]))
+        u_mx[last] = new_u_mx()
+        quantise_u(u_mx[last], u_grouped[last], slice(0, 1))
+        finish(last - 1, o_parts[last - 1])
+        quantise_u(u_mx[last], u_grouped[last], slice(1, ROW_TILES))
+        o_banks = [psum_u.tile([P, L], F32, name="last_o_bank", tag="u_bank") for m in all_m]
+        stage_two([bank[:] for bank in o_banks], u_mx[last], in2_mx[last])
+        for m in all_m:
+            result = result_pool.tile([P, L], F32, name="last_result", tag="last_result")
+            add_affine(result[:], last, m, o_banks[m][:])
+            nc.sync.dma_start(out=out[last, m * P : (m + 1) * P, :, 0], in_=result[:])

@@ -19,6 +19,7 @@ ROW_TILES = L // P
 PAIR = 2
 RUN = 16
 HALVES = PACK // PAIR
+WARM_UP = 4
 AHEAD = 4
 
 FLOPS = 2 * B * L * D * D + 2 * B * L * L * D
@@ -201,11 +202,7 @@ def tile_biaffine_2_pa_t_kernel(tc, input1, input2, w1, aff1, aff2, bias, out):
 
         aff_rows = const.tile([P, P], BF16, name="aff_rows")
         nc.vector.memset(aff_rows[:], 0.0)
-        nc.sync.dma_start(
-            out=aff_rows[0 : B * ROW_TILES, :], in_=aff1.rearrange("b (m p) o -> (b m) (p o)", p=P)
-        )
         bias_bf16 = const.tile([P, 1], BF16, name="bias_bf16")
-        nc.sync.dma_start(out=bias_bf16[:], in_=bias.partition_broadcast(P))
 
         w_raw = {(0, g1): load_w_block(0, g1) for g1 in range(PASSES)}
         in1_raw[0] = load_tokens(input1[0], "in1_raw")
@@ -216,16 +213,11 @@ def tile_biaffine_2_pa_t_kernel(tc, input1, input2, w1, aff1, aff2, bias, out):
             load_in1(n + 2)
             load_in2(n)
             if n == 1:
+                nc.sync.dma_start(
+                    out=aff_rows[0 : B * ROW_TILES, :], in_=aff1.rearrange("b (m p) o -> (b m) (p o)", p=P)
+                )
+                nc.sync.dma_start(out=bias_bf16[:], in_=bias.partition_broadcast(P))
                 nc.sync.dma_start(out=aff2_all[:], in_=aff2.rearrange("b y o -> (b y o)").partition_broadcast(P))
-
-        aff_bank = psum_o.tile([P, P], BF16, name="aff_bank", tag="o_bank")
-        nc.tensor.transpose(aff_bank[:], aff_rows[:], ident_bf16[:])
-        bias_f32 = const.tile([P, 1], F32, name="bias_f32")
-        nc.vector.tensor_copy(out=bias_f32[:], in_=bias_bf16[:])
-        aff1_col = const.tile([P, B * ROW_TILES], F32, name="aff1_col")
-        nc.vector.tensor_scalar(
-            out=aff1_col[:], in0=aff_bank[:, 0 : B * ROW_TILES], scalar1=bias_f32[:, 0:1], scalar2=None, op0=ADD
-        )
 
         in1_mx = {}
         in2_mx = {}
@@ -261,6 +253,11 @@ def tile_biaffine_2_pa_t_kernel(tc, input1, input2, w1, aff1, aff2, bias, out):
 
         w_grouped = group_w(0)
         in1_grouped = group_tokens(transpose_tokens(in1_raw[0]), 0, "in1_grouped")
+        warm_bank = psum_o.tile([P, ROW_TILES * L], F32, name="warm_bank", tag="o_bank")
+        for step in range(WARM_UP):
+            nc.tensor.matmul(
+                warm_bank[:], lhsT=ident_bf16[:], rhs=in1_raw[0][:, 0, 0 : ROW_TILES * L], start=True, stop=True
+            )
         quantise_w(0, w_grouped)
         w_grouped = group_w(1)
         in1_mx[0] = quantise(in1_grouped[:].rearrange("p g c -> p (g c)"), "in1")
@@ -277,6 +274,15 @@ def tile_biaffine_2_pa_t_kernel(tc, input1, input2, w1, aff1, aff2, bias, out):
         in2_grouped = group_tokens(transpose_ordered(in2_ordered[0]), 2, "in2_grouped")
         in2_ordered[1] = order_in2(in2_raw[1])
         in2_mx[0] = quantise(in2_grouped[:].rearrange("p g c -> p (g c)"), "in2")
+
+        aff_bank = psum_o.tile([P, P], BF16, name="aff_bank", tag="o_bank")
+        nc.tensor.transpose(aff_bank[:], aff_rows[:], ident_bf16[:])
+        bias_f32 = const.tile([P, 1], F32, name="bias_f32")
+        nc.vector.tensor_copy(out=bias_f32[:], in_=bias_bf16[:])
+        aff1_col = const.tile([P, B * ROW_TILES], F32, name="aff1_col")
+        nc.vector.tensor_scalar(
+            out=aff1_col[:], in0=aff_bank[:, 0 : B * ROW_TILES], scalar1=bias_f32[:, 0:1], scalar2=None, op0=ADD
+        )
 
         def by_row_tile(m_range):
             return [(m, g2) for m in m_range for g2 in range(PASSES)]

@@ -35,8 +35,7 @@ def tile_biaffine_2_pa_t_kernel(tc, input1, input2, w1, aff1, aff2, bias, out):
         grouped_pool = ctx.enter_context(tc.tile_pool(name="grouped", bufs=3))
         codes_pool = ctx.enter_context(tc.tile_pool(name="codes", bufs=3))
         result_pool = ctx.enter_context(tc.tile_pool(name="result", bufs=3))
-        psum_t = ctx.enter_context(tc.psum_pool(name="psum_t", bufs=4))
-        psum_u = ctx.enter_context(tc.psum_pool(name="psum_u", bufs=3))
+        psum_tu = ctx.enter_context(tc.psum_pool(name="psum_tu", bufs=7))
         psum_o = ctx.enter_context(tc.psum_pool(name="psum_o", bufs=1))
         ctx.enter_context(tc.manual_schedule())
 
@@ -88,7 +87,7 @@ def tile_biaffine_2_pa_t_kernel(tc, input1, input2, w1, aff1, aff2, bias, out):
         def transpose_ordered(ordered):
             banks = []
             for g in range(PASSES):
-                t_bank = psum_t.tile([P, ROW_TILES, HALVES, P], F32, name="t_bank", tag="t_bank")
+                t_bank = psum_tu.tile([P, ROW_TILES, HALVES, P], F32, name="t_bank", tag="bank")
                 for r in range(ROW_TILES):
                     for u in range(HALVES):
                         nc.tensor.transpose(t_bank[:, r, u, :], ordered[:, r, g, u, :], ident_f32[:])
@@ -99,7 +98,7 @@ def tile_biaffine_2_pa_t_kernel(tc, input1, input2, w1, aff1, aff2, bias, out):
             words = raw[:].bitcast(F32)
             banks = []
             for g in range(PASSES):
-                t_bank = psum_t.tile([P, ROW_TILES, HALVES, P], F32, name="t_bank", tag="t_bank")
+                t_bank = psum_tu.tile([P, ROW_TILES, HALVES, P], F32, name="t_bank", tag="bank")
                 for r in range(ROW_TILES):
                     for u in range(HALVES):
                         first = g * HALVES * P + u
@@ -137,7 +136,7 @@ def tile_biaffine_2_pa_t_kernel(tc, input1, input2, w1, aff1, aff2, bias, out):
             in1_codes, in1_scales = in1_mx
             for m, g2 in order:
                 x_cols = slice(m * P, (m + 1) * P)
-                u_bank = psum_u.tile([P, PACK, P], F32, name="u_bank", tag="u_bank")
+                u_bank = psum_tu.tile([P, PACK, P], F32, name="u_bank", tag="bank")
                 for t2 in range(PACK):
                     for g1 in range(PASSES):
                         nc.tensor.matmul_mx(
@@ -271,8 +270,8 @@ def tile_biaffine_2_pa_t_kernel(tc, input1, input2, w1, aff1, aff2, bias, out):
         load_in2(AHEAD)
         u_grouped[0] = new_u_grouped()
         stage_one(u_grouped[0], in1_mx[0], [(m, g2) for g2 in range(PASSES) for m in range(ROW_TILES)])
-        in2_grouped = group_tokens(transpose_ordered(in2_ordered[0]), 2, "in2_grouped")
         in2_ordered[1] = order_in2(in2_raw[1])
+        in2_grouped = group_tokens(transpose_ordered(in2_ordered[0]), 2, "in2_grouped")
         in2_mx[0] = quantise(in2_grouped[:].rearrange("p g c -> p (g c)"), "in2")
 
         aff_bank = psum_o.tile([P, P], BF16, name="aff_bank", tag="o_bank")
@@ -321,7 +320,7 @@ def tile_biaffine_2_pa_t_kernel(tc, input1, input2, w1, aff1, aff2, bias, out):
         quantise_u(u_mx[last], u_grouped[last], slice(0, 1))
         finish(last - 1, o_parts[last - 1])
         quantise_u(u_mx[last], u_grouped[last], slice(1, ROW_TILES))
-        o_banks = [psum_u.tile([P, L], F32, name="last_o_bank", tag="u_bank") for m in all_m]
+        o_banks = [psum_tu.tile([P, L], F32, name="last_o_bank", tag="bank") for m in all_m]
         stage_two([bank[:] for bank in o_banks], u_mx[last], in2_mx[last])
         for m in all_m:
             result = result_pool.tile([P, L], F32, name="last_result", tag="last_result")

@@ -31,16 +31,14 @@ def tile_biaffine_2_pa_t_kernel(tc, input1, input2, w1, aff1, aff2, bias, out):
         const = ctx.enter_context(tc.tile_pool(name="const", bufs=1))
         w_stage = ctx.enter_context(tc.tile_pool(name="w_stage", bufs=PASSES * PASSES))
         raw_pool = ctx.enter_context(tc.tile_pool(name="raw", bufs=AHEAD + 2))
-        ordered_pool = ctx.enter_context(tc.tile_pool(name="ordered", bufs=2))
+        ordered_pool = ctx.enter_context(tc.tile_pool(name="ordered", bufs=4))
         grouped_pool = ctx.enter_context(tc.tile_pool(name="grouped", bufs=3))
-        codes_pool = ctx.enter_context(tc.tile_pool(name="codes", bufs=3))
+        codes_pool = ctx.enter_context(tc.tile_pool(name="codes", bufs=4))
         result_pool = ctx.enter_context(tc.tile_pool(name="result", bufs=3))
         psum_tu = ctx.enter_context(tc.psum_pool(name="psum_tu", bufs=7))
         psum_o = ctx.enter_context(tc.psum_pool(name="psum_o", bufs=1))
         ctx.enter_context(tc.manual_schedule())
 
-        def bank_copy(index):
-            return nc.vector.tensor_copy if index == 3 else nc.scalar.copy
 
         def load_tokens(tokens, name):
             raw = raw_pool.tile([P, ROW_TILES, D], BF16, name=name, tag=name)
@@ -107,11 +105,12 @@ def tile_biaffine_2_pa_t_kernel(tc, input1, input2, w1, aff1, aff2, bias, out):
                 banks.append(t_bank)
             return banks
 
-        def group_tokens(banks, first_index, name):
+        def group_tokens(banks, vector_passes, name):
             grouped = grouped_pool.tile([P, PASSES, L * PACK], BF16, name=name, tag=name, align_bytes=64)
             grouped_words = grouped[:].bitcast(F32)
             for g in range(PASSES):
-                bank_copy(first_index + g)(
+                copy = nc.vector.tensor_copy if g in vector_passes else nc.scalar.copy
+                copy(
                     out=grouped_words[:, g, :].rearrange("p (q r u) -> p q r u", r=ROW_TILES, u=HALVES),
                     in_=banks[g][:].rearrange("p r u q -> p q r u"),
                 )
@@ -251,7 +250,7 @@ def tile_biaffine_2_pa_t_kernel(tc, input1, input2, w1, aff1, aff2, bias, out):
                 )
 
         w_grouped = group_w(0)
-        in1_grouped = group_tokens(transpose_tokens(in1_raw[0]), 0, "in1_grouped")
+        in1_grouped = group_tokens(transpose_tokens(in1_raw[0]), (), "in1_grouped")
         warm_bank = psum_o.tile([P, ROW_TILES * L], F32, name="warm_bank", tag="o_bank")
         for step in range(WARM_UP):
             nc.tensor.matmul(
@@ -262,7 +261,7 @@ def tile_biaffine_2_pa_t_kernel(tc, input1, input2, w1, aff1, aff2, bias, out):
         in1_mx[0] = quantise(in1_grouped[:].rearrange("p g c -> p (g c)"), "in1")
         quantise_w(1, w_grouped)
 
-        in1_grouped = group_tokens(transpose_tokens(in1_raw[1]), 0, "in1_grouped")
+        in1_grouped = group_tokens(transpose_tokens(in1_raw[1]), (), "in1_grouped")
         in2_ordered = {0: order_in2(in2_raw[0])}
         in1_mx[1] = quantise(in1_grouped[:].rearrange("p g c -> p (g c)"), "in1")
         in1_ordered = {2: order_in1(in1_raw[2])}
@@ -271,7 +270,7 @@ def tile_biaffine_2_pa_t_kernel(tc, input1, input2, w1, aff1, aff2, bias, out):
         u_grouped[0] = new_u_grouped()
         stage_one(u_grouped[0], in1_mx[0], [(m, g2) for g2 in range(PASSES) for m in range(ROW_TILES)])
         in2_ordered[1] = order_in2(in2_raw[1])
-        in2_grouped = group_tokens(transpose_ordered(in2_ordered[0]), 2, "in2_grouped")
+        in2_grouped = group_tokens(transpose_ordered(in2_ordered[0]), (1,), "in2_grouped")
         in2_mx[0] = quantise(in2_grouped[:].rearrange("p g c -> p (g c)"), "in2")
 
         aff_bank = psum_o.tile([P, P], BF16, name="aff_bank", tag="o_bank")
@@ -288,34 +287,91 @@ def tile_biaffine_2_pa_t_kernel(tc, input1, input2, w1, aff1, aff2, bias, out):
 
         all_m = range(ROW_TILES)
         last = B - 1
-        for n in range(1, B):
-            if n + 2 < B:
-                in1_ordered[n + 2] = order_in1(in1_raw[n + 2])
-            u_mx[n - 1] = new_u_mx()
-            quantise_u(u_mx[n - 1], u_grouped[n - 1], slice(0, ROW_TILES))
-            if n + 1 < B:
-                in2_ordered[n + 1] = order_in2(in2_raw[n + 1])
-            if n >= 2:
-                finish(n - 2, o_parts[n - 2])
-            load_in1(n + AHEAD + 2)
-            load_in2(n + AHEAD)
-            banks = []
-            if n < last:
-                banks = transpose_ordered(in1_ordered[n + 1])
-            banks = banks + transpose_ordered(in2_ordered[n])
-            if n < last:
-                in1_grouped = group_tokens(banks[0:PASSES], 0, "in1_grouped")
-            in2_grouped = group_tokens(banks[-PASSES:], 2, "in2_grouped")
-            if n < last:
-                in1_mx[n + 1] = quantise(in1_grouped[:].rearrange("p g c -> p (g c)"), "in1")
-            in2_mx[n] = quantise(in2_grouped[:].rearrange("p g c -> p (g c)"), "in2")
-            u_grouped[n] = new_u_grouped()
-            stage_one(u_grouped[n], in1_mx[n], by_row_tile(all_m if n < last else all_m[:1]))
+        in1_grouped = {}
+        in2_grouped = {}
+
+        def sort_in1(k):
+            if k < B:
+                in1_ordered[k] = order_in1(in1_raw[k])
+
+        def sort_in2(k):
+            if k < B:
+                in2_ordered[k] = order_in2(in2_raw[k])
+
+        def turn_in1(k, vector_passes):
+            if k < B:
+                in1_grouped[k] = group_tokens(transpose_ordered(in1_ordered[k]), vector_passes, "in1_grouped")
+
+        def turn_in2(k, vector_passes):
+            in2_grouped[k] = group_tokens(transpose_ordered(in2_ordered[k]), vector_passes, "in2_grouped")
+
+        def quantise_in1(k):
+            if k < B:
+                in1_mx[k] = quantise(in1_grouped[k][:].rearrange("p g c -> p (g c)"), "in1")
+
+        def quantise_in2(k):
+            in2_mx[k] = quantise(in2_grouped[k][:].rearrange("p g c -> p (g c)"), "in2")
+
+        def quantise_whole_u(k):
+            u_mx[k] = new_u_mx()
+            quantise_u(u_mx[k], u_grouped[k], slice(0, ROW_TILES))
+
+        def whole_stage_one(k):
+            u_grouped[k] = new_u_grouped()
+            stage_one(u_grouped[k], in1_mx[k], by_row_tile(all_m))
+
+        def whole_stage_two(k):
             o_bank = psum_o.tile([P, ROW_TILES, L], F32, name="o_bank", tag="o_bank")
-            o_parts[n - 1] = [o_bank[:, m, :] for m in all_m]
-            stage_two(o_parts[n - 1], u_mx[n - 1], in2_mx[n - 1])
+            o_parts[k] = [o_bank[:, m, :] for m in all_m]
+            stage_two(o_parts[k], u_mx[k], in2_mx[k])
+
+        sort_in1(3)
+        turn_in1(2, ())
+        turn_in2(1, (1,))
+        sort_in1(4)
+        quantise_in1(2)
+        quantise_in2(1)
+        sort_in2(2)
+        sort_in2(3)
+        load_in1(AHEAD + 3)
+        load_in2(AHEAD + 1)
+        whole_stage_one(1)
+
+        for n in range(2, B, 2):
+            quantise_whole_u(n - 2)
+            if n > 2:
+                finish(n - 3, o_parts[n - 3])
+            sort_in1(n + 3)
+            turn_in1(n + 1, ())
+            turn_in1(n + 2, (0,))
+            sort_in1(n + 4)
+            quantise_whole_u(n - 1)
+            turn_in2(n, (1,))
+            turn_in2(n + 1, ())
+            quantise_in1(n + 1)
+            quantise_in1(n + 2)
+            quantise_in2(n)
+            quantise_in2(n + 1)
+            for k in (n, n + 1):
+                load_in1(k + AHEAD + 2)
+                load_in2(k + AHEAD)
+            whole_stage_one(n)
+            whole_stage_two(n - 2)
+            finish(n - 2, o_parts[n - 2])
+            sort_in2(n + 2)
+            sort_in2(n + 3)
+            if n + 1 < last:
+                whole_stage_one(n + 1)
+                whole_stage_two(n - 1)
+
+        u_grouped[last] = new_u_grouped()
+        stage_one(u_grouped[last], in1_mx[last], by_row_tile(all_m[:1]))
+        whole_stage_two(last - 2)
+        quantise_whole_u(last - 1)
+        finish(last - 2, o_parts[last - 2])
 
         stage_one(u_grouped[last], in1_mx[last], by_row_tile(all_m[1:]))
+        whole_stage_two(last - 1)
         u_mx[last] = new_u_mx()
         quantise_u(u_mx[last], u_grouped[last], slice(0, 1))
         finish(last - 1, o_parts[last - 1])

@@ -17,10 +17,11 @@ K_PASS = P * PACK
 PASSES = D // K_PASS
 ROW_TILES = L // P
 PAIR = 2
-RUN = 16
 HALVES = PACK // PAIR
+RUN = 16
+SLOTS = 2
 WARM_UP = 4
-AHEAD = 4
+AHEAD = 3
 
 FLOPS = 2 * B * L * D * D + 2 * B * L * L * D
 
@@ -30,31 +31,43 @@ def tile_biaffine_2_pa_t_kernel(tc, input1, input2, w1, aff1, aff2, bias, out):
     with ExitStack() as ctx:
         const = ctx.enter_context(tc.tile_pool(name="const", bufs=1))
         w_stage = ctx.enter_context(tc.tile_pool(name="w_stage", bufs=PASSES * PASSES))
-        raw_pool = ctx.enter_context(tc.tile_pool(name="raw", bufs=AHEAD + 2))
-        ordered_pool = ctx.enter_context(tc.tile_pool(name="ordered", bufs=4))
-        grouped_pool = ctx.enter_context(tc.tile_pool(name="grouped", bufs=3))
-        codes_pool = ctx.enter_context(tc.tile_pool(name="codes", bufs=4))
+        w_group = ctx.enter_context(tc.tile_pool(name="w_group", bufs=PASSES))
+        raw_pool = ctx.enter_context(tc.tile_pool(name="raw", bufs=AHEAD))
+        ordered_pool = ctx.enter_context(tc.tile_pool(name="ordered", bufs=2))
+        grouped_pool = ctx.enter_context(tc.tile_pool(name="grouped", bufs=2))
+        codes_pool = ctx.enter_context(tc.tile_pool(name="codes", bufs=3))
+        u_codes_pool = ctx.enter_context(tc.tile_pool(name="u_codes", bufs=2))
         result_pool = ctx.enter_context(tc.tile_pool(name="result", bufs=3))
         psum_tu = ctx.enter_context(tc.psum_pool(name="psum_tu", bufs=7))
         psum_o = ctx.enter_context(tc.psum_pool(name="psum_o", bufs=1))
         ctx.enter_context(tc.manual_schedule())
 
+        def in1_place(k):
+            return (k + 1) // SLOTS, (k + 1) % SLOTS
 
-        def load_tokens(tokens, name):
-            raw = raw_pool.tile([P, ROW_TILES, D], BF16, name=name, tag=name)
-            nc.sync.dma_start(out=raw[:], in_=tokens.rearrange("(q r) k -> q r k", r=ROW_TILES))
-            return raw
+        def in2_place(k):
+            return k // SLOTS, k % SLOTS
 
-        in1_raw = {}
-        in2_raw = {}
+        both = slice(0, SLOTS)
+
+        raw = {}
+
+        def load_tokens(name, tokens, place):
+            j, s = place
+            if (name, j) not in raw:
+                raw_tile = raw_pool.tile([P, SLOTS, ROW_TILES, D], BF16, name=name + "_raw", tag=name + "_raw")
+                raw[name, j] = raw_tile
+            nc.sync.dma_start(
+                out=raw[name, j][:, s], in_=tokens.rearrange("(q r) k -> q r k", r=ROW_TILES)
+            )
 
         def load_in1(k):
             if k < B:
-                in1_raw[k] = load_tokens(input1[k], "in1_raw")
+                load_tokens("in1", input1[k], in1_place(k))
 
         def load_in2(k):
             if k < B:
-                in2_raw[k] = load_tokens(input2[k], "in2_raw")
+                load_tokens("in2", input2[k], in2_place(k))
 
         def load_w_block(g2, g1):
             w_raw = w_stage.tile([P, PACK, K_PASS], BF16, name="w_raw", tag="w_raw")
@@ -66,73 +79,84 @@ def tile_biaffine_2_pa_t_kernel(tc, input1, input2, w1, aff1, aff2, bias, out):
             )
             return w_raw
 
-        def order_in1(raw):
-            ordered = ordered_pool.tile([P, ROW_TILES, PASSES, HALVES, P], F32, name="in1_ordered", tag="in1_ordered")
-            nc.vector.tensor_copy(
-                out=ordered[:],
-                in_=raw[:].bitcast(F32).rearrange("q r (g p u) -> q r g u p", g=PASSES, u=HALVES),
-            )
-            return ordered
+        ordered = {}
+        grouped = {}
+        codes = {}
 
-        def order_in2(raw):
-            ordered = ordered_pool.tile([P, ROW_TILES, PASSES, HALVES, P], F32, name="in2_ordered", tag="in2_ordered")
-            nc.vector.tensor_copy(
-                out=ordered[:].bitcast(BF16).rearrange("q r g u (d i) -> q (r g) u d i", i=RUN),
-                in_=raw[:].rearrange("q r (g d u i) -> q (r g) u d i", g=PASSES, u=HALVES, i=RUN),
-            )
-            return ordered
+        def new_ordered(name, j):
+            if (name, j) not in ordered:
+                ordered_tile = ordered_pool.tile(
+                    [P, SLOTS, ROW_TILES, PASSES, HALVES, P], F32, name=name + "_ordered", tag=name + "_ordered"
+                )
+                ordered[name, j] = ordered_tile
+            return ordered[name, j]
 
-        def transpose_ordered(ordered):
+        def sort_in1(j, slots):
+            nc.vector.tensor_copy(
+                out=new_ordered("in1", j)[:, slots].rearrange("q s r g u p -> q (s r g) u p"),
+                in_=raw["in1", j][:, slots].bitcast(F32).rearrange("q s r (g p u) -> q (s r g) u p", g=PASSES, u=HALVES),
+            )
+
+        def sort_in2(j, slots):
+            nc.vector.tensor_copy(
+                out=new_ordered("in2", j)[:, slots].bitcast(BF16).rearrange("q s r g u (d i) -> q (s r g) u d i", i=RUN),
+                in_=raw["in2", j][:, slots].rearrange("q s r (g d u i) -> q (s r g) u d i", g=PASSES, u=HALVES, i=RUN),
+            )
+
+        def turn(name, j, s, vector_passes, stepped=False):
+            if (name, j) not in grouped:
+                grouped_tile = grouped_pool.tile(
+                    [P, SLOTS, PASSES, L * PACK], BF16, name=name + "_grouped", tag=name + "_grouped", align_bytes=64
+                )
+                grouped[name, j] = grouped_tile
+            grouped_words = grouped[name, j][:, s].bitcast(F32)
             banks = []
             for g in range(PASSES):
                 t_bank = psum_tu.tile([P, ROW_TILES, HALVES, P], F32, name="t_bank", tag="bank")
                 for r in range(ROW_TILES):
                     for u in range(HALVES):
-                        nc.tensor.transpose(t_bank[:, r, u, :], ordered[:, r, g, u, :], ident_f32[:])
+                        if stepped:
+                            first = g * HALVES * P + u
+                            words = raw[name, j][:, s, r].bitcast(F32)[:, first : (g + 1) * HALVES * P : HALVES]
+                        else:
+                            words = ordered[name, j][:, s, r, g, u, :]
+                        nc.tensor.transpose(t_bank[:, r, u, :], words, ident_f32[:])
                 banks.append(t_bank)
-            return banks
-
-        def transpose_tokens(raw):
-            words = raw[:].bitcast(F32)
-            banks = []
-            for g in range(PASSES):
-                t_bank = psum_tu.tile([P, ROW_TILES, HALVES, P], F32, name="t_bank", tag="bank")
-                for r in range(ROW_TILES):
-                    for u in range(HALVES):
-                        first = g * HALVES * P + u
-                        last = (g + 1) * HALVES * P
-                        nc.tensor.transpose(t_bank[:, r, u, :], words[:, r, first:last:HALVES], ident_f32[:])
-                banks.append(t_bank)
-            return banks
-
-        def group_tokens(banks, vector_passes, name):
-            grouped = grouped_pool.tile([P, PASSES, L * PACK], BF16, name=name, tag=name, align_bytes=64)
-            grouped_words = grouped[:].bitcast(F32)
             for g in range(PASSES):
                 copy = nc.vector.tensor_copy if g in vector_passes else nc.scalar.copy
                 copy(
                     out=grouped_words[:, g, :].rearrange("p (q r u) -> p q r u", r=ROW_TILES, u=HALVES),
                     in_=banks[g][:].rearrange("p r u q -> p q r u"),
                 )
-            return grouped
 
-        def quantise(grouped_flat, name):
-            codes = codes_pool.tile([P, PASSES, L], U32, name=name + "_codes", tag=name + "_codes", align_bytes=64)
-            scales = codes_pool.tile([P, PASSES, L], U8, name=name + "_scales", tag=name + "_scales", align_bytes=64)
+        def quantise(name, j, slots):
+            if (name, j) not in codes:
+                code_tile = codes_pool.tile(
+                    [P, SLOTS, PASSES, L], U32, name=name + "_codes", tag=name + "_codes", align_bytes=64
+                )
+                scale_tile = codes_pool.tile(
+                    [P, SLOTS, PASSES, L], U8, name=name + "_scales", tag=name + "_scales", align_bytes=64
+                )
+                codes[name, j] = (code_tile, scale_tile)
+            code_tile, scale_tile = codes[name, j]
             nc.vector.quantize_mx(
-                out=codes[:].rearrange("p g c -> p (g c)").bitcast(FP8X4),
-                scales=scales[:].rearrange("p g c -> p (g c)"),
-                in_=grouped_flat,
-            )
-            return codes, scales
-
-        def new_u_grouped():
-            return grouped_pool.tile(
-                [P, ROW_TILES, PASSES, P, PACK], BF16, name="u_grouped", tag="u_grouped", align_bytes=64
+                out=code_tile[:, slots].rearrange("p s g c -> p (s g c)").bitcast(FP8X4),
+                scales=scale_tile[:, slots].rearrange("p s g c -> p (s g c)"),
+                in_=grouped[name, j][:, slots].rearrange("p s g c -> p (s g c)"),
             )
 
-        def stage_one(u_grouped, in1_mx, order):
-            in1_codes, in1_scales = in1_mx
+        u_grouped = {}
+        u_codes = {}
+
+        def stage_one(b, order):
+            j, s = in2_place(b)
+            if j not in u_grouped:
+                u_tile = grouped_pool.tile(
+                    [P, SLOTS, ROW_TILES, PASSES, P, PACK], BF16, name="u_grouped", tag="u_grouped", align_bytes=64
+                )
+                u_grouped[j] = u_tile
+            in1_j, in1_s = in1_place(b)
+            in1_codes, in1_scales = codes["in1", in1_j]
             for m, g2 in order:
                 x_cols = slice(m * P, (m + 1) * P)
                 u_bank = psum_tu.tile([P, PACK, P], F32, name="u_bank", tag="bank")
@@ -142,37 +166,41 @@ def tile_biaffine_2_pa_t_kernel(tc, input1, input2, w1, aff1, aff2, bias, out):
                             out=u_bank[:, t2, :],
                             lhsT=w_codes[:, g2, t2, g1, :].bitcast(FP8X4),
                             lhsT_scale=w_scales[:, g2, t2, g1, :],
-                            rhs=in1_codes[:, g1, x_cols].bitcast(FP8X4),
-                            rhs_scale=in1_scales[:, g1, x_cols],
+                            rhs=in1_codes[:, in1_s, g1, x_cols].bitcast(FP8X4),
+                            rhs_scale=in1_scales[:, in1_s, g1, x_cols],
                             start=(g1 == 0),
                             stop=(g1 == PASSES - 1),
                         )
-                nc.scalar.copy(out=u_grouped[:, m, g2], in_=u_bank[:].rearrange("p t x -> p x t"))
+                nc.scalar.copy(out=u_grouped[j][:, s, m, g2], in_=u_bank[:].rearrange("p t x -> p x t"))
 
-        def new_u_mx():
-            codes = codes_pool.tile([P, ROW_TILES, PASSES, P], U32, name="u_codes", tag="u_codes", align_bytes=64)
-            scales = codes_pool.tile([P, ROW_TILES, PASSES, P], U8, name="u_scales", tag="u_scales", align_bytes=64)
-            return codes, scales
-
-        def quantise_u(u_mx, u_grouped, m_part):
-            codes, scales = u_mx
+        def quantise_u(j, slots, m_part):
+            if j not in u_codes:
+                code_tile = u_codes_pool.tile(
+                    [P, SLOTS, ROW_TILES, PASSES, P], U32, name="u_codes", tag="u_codes", align_bytes=64
+                )
+                scale_tile = u_codes_pool.tile(
+                    [P, SLOTS, ROW_TILES, PASSES, P], U8, name="u_scales", tag="u_scales", align_bytes=64
+                )
+                u_codes[j] = (code_tile, scale_tile)
+            code_tile, scale_tile = u_codes[j]
             nc.vector.quantize_mx(
-                out=codes[:, m_part].rearrange("p m g x -> p (m g x)").bitcast(FP8X4),
-                scales=scales[:, m_part].rearrange("p m g x -> p (m g x)"),
-                in_=u_grouped[:, m_part].rearrange("p m g x t -> p (m g x t)"),
+                out=code_tile[:, slots, m_part].rearrange("p s m g x -> p (s m g x)").bitcast(FP8X4),
+                scales=scale_tile[:, slots, m_part].rearrange("p s m g x -> p (s m g x)"),
+                in_=u_grouped[j][:, slots, m_part].rearrange("p s m g x t -> p (s m g x t)"),
             )
 
-        def stage_two(o_parts, u_mx, in2_mx):
-            u_codes, u_scales = u_mx
-            in2_codes, in2_scales = in2_mx
+        def stage_two(b, o_parts):
+            j, s = in2_place(b)
+            u_code_tile, u_scale_tile = u_codes[j]
+            in2_codes, in2_scales = codes["in2", j]
             for m in range(ROW_TILES):
                 for g2 in range(PASSES):
                     nc.tensor.matmul_mx(
                         out=o_parts[m],
-                        lhsT=u_codes[:, m, g2, :].bitcast(FP8X4),
-                        lhsT_scale=u_scales[:, m, g2, :],
-                        rhs=in2_codes[:, g2, :].bitcast(FP8X4),
-                        rhs_scale=in2_scales[:, g2, :],
+                        lhsT=u_code_tile[:, s, m, g2, :].bitcast(FP8X4),
+                        lhsT_scale=u_scale_tile[:, s, m, g2, :],
+                        rhs=in2_codes[:, s, g2, :].bitcast(FP8X4),
+                        rhs_scale=in2_scales[:, s, g2, :],
                         start=(g2 == 0),
                         stop=(g2 == PASSES - 1),
                     )
@@ -187,91 +215,107 @@ def tile_biaffine_2_pa_t_kernel(tc, input1, input2, w1, aff1, aff2, bias, out):
                 op1=ADD,
             )
 
-        def finish(b, o_parts):
+        o_banks = {}
+
+        def whole_stage_two(b):
+            o_bank = psum_o.tile([P, ROW_TILES, L], F32, name="o_bank", tag="o_bank")
+            o_banks[b] = o_bank
+            stage_two(b, [o_bank[:, m, :] for m in range(ROW_TILES)])
+
+        def finish(b):
             result = result_pool.tile([P, ROW_TILES, L], F32, name="result", tag="result")
             for m in range(ROW_TILES):
-                add_affine(result[:, m, :], b, m, o_parts[m])
+                add_affine(result[:, m, :], b, m, o_banks[b][:, m, :])
             nc.sync.dma_start(out=out[b].rearrange("(m p) y o -> p m (y o)", p=P), in_=result[:])
 
         ident_f32 = const.tile([P, P], F32, name="ident_f32")
         make_identity(nc, ident_f32[:])
         ident_bf16 = const.tile([P, P], BF16, name="ident_bf16")
         make_identity(nc, ident_bf16[:])
-
         aff_rows = const.tile([P, P], BF16, name="aff_rows")
         nc.vector.memset(aff_rows[:], 0.0)
         bias_bf16 = const.tile([P, 1], BF16, name="bias_bf16")
-
-        w_raw = {(0, g1): load_w_block(0, g1) for g1 in range(PASSES)}
-        in1_raw[0] = load_tokens(input1[0], "in1_raw")
         aff2_all = const.tile([P, B * L], BF16, name="aff2_all")
-        w_raw.update({(1, g1): load_w_block(1, g1) for g1 in range(PASSES)})
-        in1_raw[1] = load_tokens(input1[1], "in1_raw")
-        for n in range(AHEAD):
-            load_in1(n + 2)
-            load_in2(n)
-            if n == 1:
-                nc.sync.dma_start(
-                    out=aff_rows[0 : B * ROW_TILES, :], in_=aff1.rearrange("b (m p) o -> (b m) (p o)", p=P)
-                )
-                nc.sync.dma_start(out=bias_bf16[:], in_=bias.partition_broadcast(P))
-                nc.sync.dma_start(out=aff2_all[:], in_=aff2.rearrange("b y o -> (b y o)").partition_broadcast(P))
 
-        in1_mx = {}
-        in2_mx = {}
-        u_grouped = {}
-        u_mx = {}
-        o_parts = {}
+        w_raw = {}
+        for g1 in range(PASSES):
+            w_raw[0, g1] = load_w_block(0, g1)
+        load_in1(0)
+        for g1 in range(PASSES):
+            w_raw[1, g1] = load_w_block(1, g1)
+        load_in1(1)
+        load_in1(2)
+        load_in2(0)
+        load_in2(1)
+        nc.sync.dma_start(
+            out=aff_rows[0 : B * ROW_TILES, :], in_=aff1.rearrange("b (m p) o -> (b m) (p o)", p=P)
+        )
+        nc.sync.dma_start(out=bias_bf16[:], in_=bias.partition_broadcast(P))
+        load_in1(3)
+        load_in1(4)
+        load_in2(2)
+        load_in2(3)
 
         w_codes = const.tile([P, PASSES, PACK, PASSES, P], U32, name="w_codes", align_bytes=64)
         w_scales = const.tile([P, PASSES, PACK, PASSES, P], U8, name="w_scales", align_bytes=64)
 
         def group_w(g2):
-            w_grouped = w_stage.tile([P, PACK, PASSES, P, PACK], BF16, name="w_grouped", tag="w_grouped", align_bytes=64)
+            w_grouped = w_group.tile([P, PACK, PASSES, P, PACK], BF16, name="w_grouped", tag="w_grouped", align_bytes=64)
+            target = w_grouped[:].rearrange(
+                "p (u e) g (d i) t -> p e g d u i t", u=HALVES, e=PAIR, i=RUN // PAIR
+            )
             for g1 in range(PASSES):
-                w_sorted = w_raw[g2, g1][:].rearrange(
-                    "p t (d u i e) -> p u e d i t", u=HALVES, i=RUN // PAIR, e=PAIR
-                )
-                for t2 in range(PACK):
-                    copy = nc.scalar.copy if t2 == 1 or (t2, g1) == (3, 0) else nc.vector.tensor_copy
-                    copy(
-                        out=w_grouped[:, t2, g1].rearrange("p (d i) t -> p d i t", i=RUN // PAIR),
-                        in_=w_sorted[:, t2 // PAIR, t2 % PAIR],
-                    )
+                source = w_raw[g2, g1][:].rearrange("p t (d u i e) -> p e d u i t", u=HALVES, i=RUN // PAIR, e=PAIR)
+                nc.vector.tensor_copy(out=target[:, 0, g1], in_=source[:, 0])
+                if g1 == 0:
+                    nc.scalar.copy(out=target[:, 1, g1], in_=source[:, 1])
+                else:
+                    nc.scalar.copy(out=target[:, 1, g1, :, 0], in_=source[:, 1, :, 0])
+                    nc.vector.tensor_copy(out=target[:, 1, g1, :, 1], in_=source[:, 1, :, 1])
             return w_grouped
 
         def quantise_w(g2, w_grouped):
-            for first in range(0, PACK, PAIR):
-                t2_pair = slice(first, first + PAIR)
-                nc.vector.quantize_mx(
-                    out=w_codes[:, g2, t2_pair].rearrange("p s g q -> p (s g q)").bitcast(FP8X4),
-                    scales=w_scales[:, g2, t2_pair].rearrange("p s g q -> p (s g q)"),
-                    in_=w_grouped[:, t2_pair].rearrange("p s g q t -> p (s g q t)"),
-                )
+            nc.vector.quantize_mx(
+                out=w_codes[:, g2].rearrange("p s g q -> p (s g q)").bitcast(FP8X4),
+                scales=w_scales[:, g2].rearrange("p s g q -> p (s g q)"),
+                in_=w_grouped[:].rearrange("p s g q t -> p (s g q t)"),
+            )
+
+        by_row_tile = [(m, g2) for m in range(ROW_TILES) for g2 in range(PASSES)]
+        by_half = [(m, g2) for g2 in range(PASSES) for m in range(ROW_TILES)]
 
         w_grouped = group_w(0)
-        in1_grouped = group_tokens(transpose_tokens(in1_raw[0]), (), "in1_grouped")
+        j, s = in1_place(0)
+        turn("in1", j, s, (), stepped=True)
         warm_bank = psum_o.tile([P, ROW_TILES * L], F32, name="warm_bank", tag="o_bank")
         for step in range(WARM_UP):
             nc.tensor.matmul(
-                warm_bank[:], lhsT=ident_bf16[:], rhs=in1_raw[0][:, 0, 0 : ROW_TILES * L], start=True, stop=True
+                warm_bank[:], lhsT=ident_bf16[:], rhs=raw["in1", j][:, s, 0, 0 : ROW_TILES * L], start=True, stop=True
             )
         quantise_w(0, w_grouped)
         w_grouped = group_w(1)
-        in1_mx[0] = quantise(in1_grouped[:].rearrange("p g c -> p (g c)"), "in1")
+        quantise("in1", j, slice(s, s + 1))
         quantise_w(1, w_grouped)
 
-        in1_grouped = group_tokens(transpose_tokens(in1_raw[1]), (), "in1_grouped")
-        in2_ordered = {0: order_in2(in2_raw[0])}
-        in1_mx[1] = quantise(in1_grouped[:].rearrange("p g c -> p (g c)"), "in1")
-        in1_ordered = {2: order_in1(in1_raw[2])}
-        load_in1(AHEAD + 2)
-        load_in2(AHEAD)
-        u_grouped[0] = new_u_grouped()
-        stage_one(u_grouped[0], in1_mx[0], [(m, g2) for g2 in range(PASSES) for m in range(ROW_TILES)])
-        in2_ordered[1] = order_in2(in2_raw[1])
-        in2_grouped = group_tokens(transpose_ordered(in2_ordered[0]), (1,), "in2_grouped")
-        in2_mx[0] = quantise(in2_grouped[:].rearrange("p g c -> p (g c)"), "in2")
+        turn("in1", 1, 0, (), stepped=True)
+        sort_in2(0, slice(0, 1))
+        quantise("in1", 1, slice(0, 1))
+        sort_in1(1, slice(1, 2))
+        stage_one(0, by_half)
+        sort_in2(0, slice(1, 2))
+        load_in1(5)
+        load_in1(6)
+        nc.sync.dma_start(out=aff2_all[:], in_=aff2.rearrange("b y o -> (b y o)").partition_broadcast(P))
+        load_in2(4)
+        load_in2(5)
+        turn("in2", 0, 0, (1,))
+        turn("in1", 1, 1, ())
+        turn("in2", 0, 1, (1,))
+        sort_in1(2, both)
+        quantise("in1", 1, slice(1, 2))
+        stage_one(1, by_row_tile)
+        sort_in2(1, both)
+        quantise("in2", 0, both)
 
         aff_bank = psum_o.tile([P, P], BF16, name="aff_bank", tag="o_bank")
         nc.tensor.transpose(aff_bank[:], aff_rows[:], ident_bf16[:])
@@ -282,103 +326,51 @@ def tile_biaffine_2_pa_t_kernel(tc, input1, input2, w1, aff1, aff2, bias, out):
             out=aff1_col[:], in0=aff_bank[:, 0 : B * ROW_TILES], scalar1=bias_f32[:, 0:1], scalar2=None, op0=ADD
         )
 
-        def by_row_tile(m_range):
-            return [(m, g2) for m in m_range for g2 in range(PASSES)]
-
-        all_m = range(ROW_TILES)
+        all_m = slice(0, ROW_TILES)
         last = B - 1
-        in1_grouped = {}
-        in2_grouped = {}
-
-        def sort_in1(k):
-            if k < B:
-                in1_ordered[k] = order_in1(in1_raw[k])
-
-        def sort_in2(k):
-            if k < B:
-                in2_ordered[k] = order_in2(in2_raw[k])
-
-        def turn_in1(k, vector_passes):
-            if k < B:
-                in1_grouped[k] = group_tokens(transpose_ordered(in1_ordered[k]), vector_passes, "in1_grouped")
-
-        def turn_in2(k, vector_passes):
-            in2_grouped[k] = group_tokens(transpose_ordered(in2_ordered[k]), vector_passes, "in2_grouped")
-
-        def quantise_in1(k):
-            if k < B:
-                in1_mx[k] = quantise(in1_grouped[k][:].rearrange("p g c -> p (g c)"), "in1")
-
-        def quantise_in2(k):
-            in2_mx[k] = quantise(in2_grouped[k][:].rearrange("p g c -> p (g c)"), "in2")
-
-        def quantise_whole_u(k):
-            u_mx[k] = new_u_mx()
-            quantise_u(u_mx[k], u_grouped[k], slice(0, ROW_TILES))
-
-        def whole_stage_one(k):
-            u_grouped[k] = new_u_grouped()
-            stage_one(u_grouped[k], in1_mx[k], by_row_tile(all_m))
-
-        def whole_stage_two(k):
-            o_bank = psum_o.tile([P, ROW_TILES, L], F32, name="o_bank", tag="o_bank")
-            o_parts[k] = [o_bank[:, m, :] for m in all_m]
-            stage_two(o_parts[k], u_mx[k], in2_mx[k])
-
-        sort_in1(3)
-        turn_in1(2, ())
-        turn_in2(1, (1,))
-        sort_in1(4)
-        quantise_in1(2)
-        quantise_in2(1)
-        sort_in2(2)
-        sort_in2(3)
-        load_in1(AHEAD + 3)
-        load_in2(AHEAD + 1)
-        whole_stage_one(1)
-
-        for n in range(2, B, 2):
-            quantise_whole_u(n - 2)
+        for n in range(2, B, SLOTS):
+            j = n // SLOTS
+            in1_slots = both if n + 2 < B else slice(0, 1)
+            if n + 4 < B:
+                sort_in1(j + 2, both)
+            elif n + 3 < B:
+                sort_in1(j + 2, slice(0, 1))
+            turn("in1", j + 1, 0, ())
+            if n + 2 < B:
+                turn("in1", j + 1, 1, (0,))
             if n > 2:
-                finish(n - 3, o_parts[n - 3])
-            sort_in1(n + 3)
-            turn_in1(n + 1, ())
-            turn_in1(n + 2, (0,))
-            sort_in1(n + 4)
-            quantise_whole_u(n - 1)
-            turn_in2(n, (1,))
-            turn_in2(n + 1, ())
-            quantise_in1(n + 1)
-            quantise_in1(n + 2)
-            quantise_in2(n)
-            quantise_in2(n + 1)
-            for k in (n, n + 1):
-                load_in1(k + AHEAD + 2)
-                load_in2(k + AHEAD)
-            whole_stage_one(n)
+                finish(n - 3)
+            quantise_u(j - 1, both, all_m)
+            turn("in2", j, 0, (1,))
+            turn("in2", j, 1, ())
+            quantise("in1", j + 1, in1_slots)
+            quantise("in2", j, both)
+            for k in (n + 5, n + 6):
+                load_in1(k)
+            for k in (n + 4, n + 5):
+                load_in2(k)
+            stage_one(n, by_row_tile)
             whole_stage_two(n - 2)
-            finish(n - 2, o_parts[n - 2])
-            sort_in2(n + 2)
-            sort_in2(n + 3)
+            finish(n - 2)
+            if n + 2 < B:
+                sort_in2(j + 1, both)
             if n + 1 < last:
-                whole_stage_one(n + 1)
+                stage_one(n + 1, by_row_tile)
                 whole_stage_two(n - 1)
 
-        u_grouped[last] = new_u_grouped()
-        stage_one(u_grouped[last], in1_mx[last], by_row_tile(all_m[:1]))
+        j, s = in2_place(last)
+        stage_one(last, by_row_tile[:PASSES])
         whole_stage_two(last - 2)
-        quantise_whole_u(last - 1)
-        finish(last - 2, o_parts[last - 2])
-
-        stage_one(u_grouped[last], in1_mx[last], by_row_tile(all_m[1:]))
+        quantise_u(j, slice(0, 1), all_m)
+        finish(last - 2)
+        stage_one(last, by_row_tile[PASSES:])
         whole_stage_two(last - 1)
-        u_mx[last] = new_u_mx()
-        quantise_u(u_mx[last], u_grouped[last], slice(0, 1))
-        finish(last - 1, o_parts[last - 1])
-        quantise_u(u_mx[last], u_grouped[last], slice(1, ROW_TILES))
-        o_banks = [psum_tu.tile([P, L], F32, name="last_o_bank", tag="bank") for m in all_m]
-        stage_two([bank[:] for bank in o_banks], u_mx[last], in2_mx[last])
-        for m in all_m:
+        quantise_u(j, slice(s, s + 1), slice(0, 1))
+        finish(last - 1)
+        quantise_u(j, slice(s, s + 1), slice(1, ROW_TILES))
+        last_o_banks = [psum_tu.tile([P, L], F32, name="last_o_bank", tag="bank") for m in range(ROW_TILES)]
+        stage_two(last, [bank[:] for bank in last_o_banks])
+        for m in range(ROW_TILES):
             result = result_pool.tile([P, L], F32, name="last_result", tag="last_result")
-            add_affine(result[:], last, m, o_banks[m][:])
+            add_affine(result[:], last, m, last_o_banks[m][:])
             nc.sync.dma_start(out=out[last, m * P : (m + 1) * P, :, 0], in_=result[:])

@@ -246,12 +246,12 @@ def tile_biaffine_2_pa_t_kernel(tc, input1, input2, w1, aff1, aff2, bias, out):
         load_in1(1)
         load_in1(2)
         load_in2(0)
+        load_in1(3)
         load_in2(1)
         nc.sync.dma_start(
             out=aff_rows[0 : B * ROW_TILES, :], in_=aff1.rearrange("b (m p) o -> (b m) (p o)", p=P)
         )
         nc.sync.dma_start(out=bias_bf16[:], in_=bias.partition_broadcast(P))
-        load_in1(3)
         load_in1(4)
         load_in2(2)
         load_in2(3)
@@ -300,18 +300,18 @@ def tile_biaffine_2_pa_t_kernel(tc, input1, input2, w1, aff1, aff2, bias, out):
         turn("in1", 1, 0, (), stepped=True)
         sort_in2(0, slice(0, 1))
         quantise("in1", 1, slice(0, 1))
-        sort_in1(1, slice(1, 2))
         stage_one(0, by_half)
+        sort_in1(2, slice(0, 1))
         sort_in2(0, slice(1, 2))
         load_in1(5)
         load_in1(6)
         nc.sync.dma_start(out=aff2_all[:], in_=aff2.rearrange("b y o -> (b y o)").partition_broadcast(P))
         load_in2(4)
         load_in2(5)
-        turn("in2", 0, 0, (1,))
-        turn("in1", 1, 1, ())
+        turn("in2", 0, 0, ())
+        turn("in1", 1, 1, (), stepped=True)
         turn("in2", 0, 1, (1,))
-        sort_in1(2, both)
+        sort_in1(2, slice(1, 2))
         quantise("in1", 1, slice(1, 2))
         stage_one(1, by_row_tile)
         sort_in2(1, both)
@@ -331,19 +331,17 @@ def tile_biaffine_2_pa_t_kernel(tc, input1, input2, w1, aff1, aff2, bias, out):
         for n in range(2, B, SLOTS):
             j = n // SLOTS
             in1_slots = both if n + 2 < B else slice(0, 1)
-            if n + 4 < B:
-                sort_in1(j + 2, both)
-            elif n + 3 < B:
-                sort_in1(j + 2, slice(0, 1))
-            turn("in1", j + 1, 0, ())
-            if n + 2 < B:
-                turn("in1", j + 1, 1, (0,))
             if n > 2:
                 finish(n - 3)
+            turn("in1", j + 1, 0, ())
             quantise_u(j - 1, both, all_m)
+            if n + 2 < B:
+                turn("in1", j + 1, 1, (0,))
             turn("in2", j, 0, (1,))
             turn("in2", j, 1, ())
             quantise("in1", j + 1, in1_slots)
+            if n + 3 < B:
+                sort_in1(j + 2, both if n + 4 < B else slice(0, 1))
             quantise("in2", j, both)
             for k in (n + 5, n + 6):
                 load_in1(k)

from contextlib import ExitStack

import concourse.mybir as mybir
from concourse.masks import make_identity

F32 = mybir.dt.float32
BF16 = mybir.dt.bfloat16
U32 = mybir.dt.uint32
U8 = mybir.dt.uint8
FP8X4 = mybir.dt.float8_e4m3fn_x4
ADD = mybir.AluOpType.add

B, L, D = 16, 256, 1024
P = 128
PACK = 4
K_PASS = P * PACK
PASSES = D // K_PASS
ROW_TILES = L // P
PAIR = 2
HALVES = PACK // PAIR
RUN = 16
SLOTS = 2
WARM_UP = 4
AHEAD = 3

FLOPS = 2 * B * L * D * D + 2 * B * L * L * D


def tile_biaffine_2_pa_t_kernel(tc, input1, input2, w1, aff1, aff2, bias, out):
    nc = tc.nc
    with ExitStack() as ctx:
        const = ctx.enter_context(tc.tile_pool(name="const", bufs=1))
        w_stage = ctx.enter_context(tc.tile_pool(name="w_stage", bufs=PASSES * PASSES))
        w_group = ctx.enter_context(tc.tile_pool(name="w_group", bufs=PASSES))
        raw_pool = ctx.enter_context(tc.tile_pool(name="raw", bufs=AHEAD))
        ordered_pool = ctx.enter_context(tc.tile_pool(name="ordered", bufs=2))
        grouped_pool = ctx.enter_context(tc.tile_pool(name="grouped", bufs=2))
        codes_pool = ctx.enter_context(tc.tile_pool(name="codes", bufs=3))
        u_codes_pool = ctx.enter_context(tc.tile_pool(name="u_codes", bufs=2))
        result_pool = ctx.enter_context(tc.tile_pool(name="result", bufs=3))
        psum_tu = ctx.enter_context(tc.psum_pool(name="psum_tu", bufs=7))
        psum_o = ctx.enter_context(tc.psum_pool(name="psum_o", bufs=1))
        ctx.enter_context(tc.manual_schedule())

        def in1_place(k):
            return (k + 1) // SLOTS, (k + 1) % SLOTS

        def in2_place(k):
            return k // SLOTS, k % SLOTS

        both = slice(0, SLOTS)

        raw = {}

        def load_tokens(name, tokens, place):
            j, s = place
            if (name, j) not in raw:
                raw_tile = raw_pool.tile([P, SLOTS, ROW_TILES, D], BF16, name=name + "_raw", tag=name + "_raw")
                raw[name, j] = raw_tile
            nc.sync.dma_start(
                out=raw[name, j][:, s], in_=tokens.rearrange("(q r) k -> q r k", r=ROW_TILES)
            )

        def load_in1(k):
            if k < B:
                load_tokens("in1", input1[k], in1_place(k))

        def load_in2(k):
            if k < B:
                load_tokens("in2", input2[k], in2_place(k))

        def load_w_block(g2, g1):
            w_raw = w_stage.tile([P, PACK, K_PASS], BF16, name="w_raw", tag="w_raw")
            nc.sync.dma_start(
                out=w_raw[:],
                in_=w1[K_PASS * g1 : K_PASS * (g1 + 1), 0, K_PASS * g2 : K_PASS * (g2 + 1)].rearrange(
                    "(q t) j -> q t j", t=PACK
                ),
            )
            return w_raw

        ordered = {}
        grouped = {}
        codes = {}

        def new_ordered(name, j):
            if (name, j) not in ordered:
                ordered_tile = ordered_pool.tile(
                    [P, SLOTS, ROW_TILES, PASSES, HALVES, P], F32, name=name + "_ordered", tag=name + "_ordered"
                )
                ordered[name, j] = ordered_tile
            return ordered[name, j]

        def sort_in1(j, slots):
            nc.vector.tensor_copy(
                out=new_ordered("in1", j)[:, slots].rearrange("q s r g u p -> q (s r g) u p"),
                in_=raw["in1", j][:, slots].bitcast(F32).rearrange("q s r (g p u) -> q (s r g) u p", g=PASSES, u=HALVES),
            )

        def sort_in2(j, slots):
            nc.vector.tensor_copy(
                out=new_ordered("in2", j)[:, slots].bitcast(BF16).rearrange("q s r g u (d i) -> q (s r g) u d i", i=RUN),
                in_=raw["in2", j][:, slots].rearrange("q s r (g d u i) -> q (s r g) u d i", g=PASSES, u=HALVES, i=RUN),
            )

        def turn(name, j, s, vector_passes, stepped=False):
            if (name, j) not in grouped:
                grouped_tile = grouped_pool.tile(
                    [P, SLOTS, PASSES, L * PACK], BF16, name=name + "_grouped", tag=name + "_grouped", align_bytes=64
                )
                grouped[name, j] = grouped_tile
            grouped_words = grouped[name, j][:, s].bitcast(F32)
            banks = []
            for g in range(PASSES):
                t_bank = psum_tu.tile([P, ROW_TILES, HALVES, P], F32, name="t_bank", tag="bank")
                for r in range(ROW_TILES):
                    for u in range(HALVES):
                        if stepped:
                            first = g * HALVES * P + u
                            words = raw[name, j][:, s, r].bitcast(F32)[:, first : (g + 1) * HALVES * P : HALVES]
                        else:
                            words = ordered[name, j][:, s, r, g, u, :]
                        nc.tensor.transpose(t_bank[:, r, u, :], words, ident_f32[:])
                banks.append(t_bank)
            for g in range(PASSES):
                copy = nc.vector.tensor_copy if g in vector_passes else nc.scalar.copy
                copy(
                    out=grouped_words[:, g, :].rearrange("p (q r u) -> p q r u", r=ROW_TILES, u=HALVES),
                    in_=banks[g][:].rearrange("p r u q -> p q r u"),
                )

        def quantise(name, j, slots):
            if (name, j) not in codes:
                code_tile = codes_pool.tile(
                    [P, SLOTS, PASSES, L], U32, name=name + "_codes", tag=name + "_codes", align_bytes=64
                )
                scale_tile = codes_pool.tile(
                    [P, SLOTS, PASSES, L], U8, name=name + "_scales", tag=name + "_scales", align_bytes=64
                )
                codes[name, j] = (code_tile, scale_tile)
            code_tile, scale_tile = codes[name, j]
            nc.vector.quantize_mx(
                out=code_tile[:, slots].rearrange("p s g c -> p (s g c)").bitcast(FP8X4),
                scales=scale_tile[:, slots].rearrange("p s g c -> p (s g c)"),
                in_=grouped[name, j][:, slots].rearrange("p s g c -> p (s g c)"),
            )

        u_grouped = {}
        u_codes = {}

        def stage_one(b, order):
            j, s = in2_place(b)
            if j not in u_grouped:
                u_tile = grouped_pool.tile(
                    [P, SLOTS, ROW_TILES, PASSES, P, PACK], BF16, name="u_grouped", tag="u_grouped", align_bytes=64
                )
                u_grouped[j] = u_tile
            in1_j, in1_s = in1_place(b)
            in1_codes, in1_scales = codes["in1", in1_j]
            for m, g2 in order:
                x_cols = slice(m * P, (m + 1) * P)
                u_bank = psum_tu.tile([P, PACK, P], F32, name="u_bank", tag="bank")
                for t2 in range(PACK):
                    for g1 in range(PASSES):
                        nc.tensor.matmul_mx(
                            out=u_bank[:, t2, :],
                            lhsT=w_codes[:, g2, t2, g1, :].bitcast(FP8X4),
                            lhsT_scale=w_scales[:, g2, t2, g1, :],
                            rhs=in1_codes[:, in1_s, g1, x_cols].bitcast(FP8X4),
                            rhs_scale=in1_scales[:, in1_s, g1, x_cols],
                            start=(g1 == 0),
                            stop=(g1 == PASSES - 1),
                        )
                nc.scalar.copy(out=u_grouped[j][:, s, m, g2], in_=u_bank[:].rearrange("p t x -> p x t"))

        def quantise_u(j, slots, m_part):
            if j not in u_codes:
                code_tile = u_codes_pool.tile(
                    [P, SLOTS, ROW_TILES, PASSES, P], U32, name="u_codes", tag="u_codes", align_bytes=64
                )
                scale_tile = u_codes_pool.tile(
                    [P, SLOTS, ROW_TILES, PASSES, P], U8, name="u_scales", tag="u_scales", align_bytes=64
                )
                u_codes[j] = (code_tile, scale_tile)
            code_tile, scale_tile = u_codes[j]
            nc.vector.quantize_mx(
                out=code_tile[:, slots, m_part].rearrange("p s m g x -> p (s m g x)").bitcast(FP8X4),
                scales=scale_tile[:, slots, m_part].rearrange("p s m g x -> p (s m g x)"),
                in_=u_grouped[j][:, slots, m_part].rearrange("p s m g x t -> p (s m g x t)"),
            )

        def stage_two(b, o_parts):
            j, s = in2_place(b)
            u_code_tile, u_scale_tile = u_codes[j]
            in2_codes, in2_scales = codes["in2", j]
            for m in range(ROW_TILES):
                for g2 in range(PASSES):
                    nc.tensor.matmul_mx(
                        out=o_parts[m],
                        lhsT=u_code_tile[:, s, m, g2, :].bitcast(FP8X4),
                        lhsT_scale=u_scale_tile[:, s, m, g2, :],
                        rhs=in2_codes[:, s, g2, :].bitcast(FP8X4),
                        rhs_scale=in2_scales[:, s, g2, :],
                        start=(g2 == 0),
                        stop=(g2 == PASSES - 1),
                    )

        def add_affine(result_part, b, m, o_part):
            nc.vector.scalar_tensor_tensor(
                out=result_part,
                in0=o_part,
                scalar=aff1_col[:, b * ROW_TILES + m : b * ROW_TILES + m + 1],
                in1=aff2_all[:, b * L : (b + 1) * L],
                op0=ADD,
                op1=ADD,
            )

        o_banks = {}

        def whole_stage_two(b):
            o_bank = psum_o.tile([P, ROW_TILES, L], F32, name="o_bank", tag="o_bank")
            o_banks[b] = o_bank
            stage_two(b, [o_bank[:, m, :] for m in range(ROW_TILES)])

        def finish(b):
            result = result_pool.tile([P, ROW_TILES, L], F32, name="result", tag="result")
            for m in range(ROW_TILES):
                add_affine(result[:, m, :], b, m, o_banks[b][:, m, :])
            nc.sync.dma_start(out=out[b].rearrange("(m p) y o -> p m (y o)", p=P), in_=result[:])

        ident_f32 = const.tile([P, P], F32, name="ident_f32")
        make_identity(nc, ident_f32[:])
        ident_bf16 = const.tile([P, P], BF16, name="ident_bf16")
        make_identity(nc, ident_bf16[:])
        aff_rows = const.tile([P, P], BF16, name="aff_rows")
        nc.vector.memset(aff_rows[:], 0.0)
        bias_bf16 = const.tile([P, 1], BF16, name="bias_bf16")
        aff2_all = const.tile([P, B * L], BF16, name="aff2_all")

        w_raw = {}
        for g1 in range(PASSES):
            w_raw[0, g1] = load_w_block(0, g1)
        load_in1(0)
        for g1 in range(PASSES):
            w_raw[1, g1] = load_w_block(1, g1)
        load_in1(1)
        load_in1(2)
        load_in2(0)
        load_in1(3)
        load_in2(1)
        nc.sync.dma_start(
            out=aff_rows[0 : B * ROW_TILES, :], in_=aff1.rearrange("b (m p) o -> (b m) (p o)", p=P)
        )
        nc.sync.dma_start(out=bias_bf16[:], in_=bias.partition_broadcast(P))
        load_in1(4)
        load_in2(2)
        load_in2(3)

        w_codes = const.tile([P, PASSES, PACK, PASSES, P], U32, name="w_codes", align_bytes=64)
        w_scales = const.tile([P, PASSES, PACK, PASSES, P], U8, name="w_scales", align_bytes=64)

        def group_w(g2):
            w_grouped = w_group.tile([P, PACK, PASSES, P, PACK], BF16, name="w_grouped", tag="w_grouped", align_bytes=64)
            target = w_grouped[:].rearrange(
                "p (u e) g (d i) t -> p e g d u i t", u=HALVES, e=PAIR, i=RUN // PAIR
            )
            for g1 in range(PASSES):
                source = w_raw[g2, g1][:].rearrange("p t (d u i e) -> p e d u i t", u=HALVES, i=RUN // PAIR, e=PAIR)
                nc.vector.tensor_copy(out=target[:, 0, g1], in_=source[:, 0])
                if g1 == 0:
                    nc.scalar.copy(out=target[:, 1, g1], in_=source[:, 1])
                else:
                    nc.scalar.copy(out=target[:, 1, g1, :, 0], in_=source[:, 1, :, 0])
                    nc.vector.tensor_copy(out=target[:, 1, g1, :, 1], in_=source[:, 1, :, 1])
            return w_grouped

        def quantise_w(g2, w_grouped):
            nc.vector.quantize_mx(
                out=w_codes[:, g2].rearrange("p s g q -> p (s g q)").bitcast(FP8X4),
                scales=w_scales[:, g2].rearrange("p s g q -> p (s g q)"),
                in_=w_grouped[:].rearrange("p s g q t -> p (s g q t)"),
            )

        by_row_tile = [(m, g2) for m in range(ROW_TILES) for g2 in range(PASSES)]
        by_half = [(m, g2) for g2 in range(PASSES) for m in range(ROW_TILES)]

        w_grouped = group_w(0)
        j, s = in1_place(0)
        turn("in1", j, s, (), stepped=True)
        warm_bank = psum_o.tile([P, ROW_TILES * L], F32, name="warm_bank", tag="o_bank")
        for step in range(WARM_UP):
            nc.tensor.matmul(
                warm_bank[:], lhsT=ident_bf16[:], rhs=raw["in1", j][:, s, 0, 0 : ROW_TILES * L], start=True, stop=True
            )
        quantise_w(0, w_grouped)
        w_grouped = group_w(1)
        quantise("in1", j, slice(s, s + 1))
        quantise_w(1, w_grouped)

        turn("in1", 1, 0, (), stepped=True)
        sort_in2(0, slice(0, 1))
        quantise("in1", 1, slice(0, 1))
        stage_one(0, by_half)
        sort_in1(2, slice(0, 1))
        sort_in2(0, slice(1, 2))
        load_in1(5)
        load_in1(6)
        nc.sync.dma_start(out=aff2_all[:], in_=aff2.rearrange("b y o -> (b y o)").partition_broadcast(P))
        load_in2(4)
        load_in2(5)
        turn("in2", 0, 0, ())
        turn("in1", 1, 1, (), stepped=True)
        turn("in2", 0, 1, (1,))
        sort_in1(2, slice(1, 2))
        quantise("in1", 1, slice(1, 2))
        stage_one(1, by_row_tile)
        sort_in2(1, both)
        quantise("in2", 0, both)

        aff_bank = psum_o.tile([P, P], BF16, name="aff_bank", tag="o_bank")
        nc.tensor.transpose(aff_bank[:], aff_rows[:], ident_bf16[:])
        bias_f32 = const.tile([P, 1], F32, name="bias_f32")
        nc.vector.tensor_copy(out=bias_f32[:], in_=bias_bf16[:])
        aff1_col = const.tile([P, B * ROW_TILES], F32, name="aff1_col")
        nc.vector.tensor_scalar(
            out=aff1_col[:], in0=aff_bank[:, 0 : B * ROW_TILES], scalar1=bias_f32[:, 0:1], scalar2=None, op0=ADD
        )

        all_m = slice(0, ROW_TILES)
        last = B - 1
        for n in range(2, B, SLOTS):
            j = n // SLOTS
            in1_slots = both if n + 2 < B else slice(0, 1)
            if n > 2:
                finish(n - 3)
            turn("in1", j + 1, 0, ())
            quantise_u(j - 1, both, all_m)
            if n + 2 < B:
                turn("in1", j + 1, 1, (0,))
            turn("in2", j, 0, (1,))
            turn("in2", j, 1, ())
            quantise("in1", j + 1, in1_slots)
            if n + 3 < B:
                sort_in1(j + 2, both if n + 4 < B else slice(0, 1))
            quantise("in2", j, both)
            for k in (n + 5, n + 6):
                load_in1(k)
            for k in (n + 4, n + 5):
                load_in2(k)
            stage_one(n, by_row_tile)
            whole_stage_two(n - 2)
            finish(n - 2)
            if n + 2 < B:
                sort_in2(j + 1, both)
            if n + 1 < last:
                stage_one(n + 1, by_row_tile)
                whole_stage_two(n - 1)

        j, s = in2_place(last)
        stage_one(last, by_row_tile[:PASSES])
        whole_stage_two(last - 2)
        quantise_u(j, slice(0, 1), all_m)
        finish(last - 2)
        stage_one(last, by_row_tile[PASSES:])
        whole_stage_two(last - 1)
        quantise_u(j, slice(s, s + 1), slice(0, 1))
        finish(last - 1)
        quantise_u(j, slice(s, s + 1), slice(1, ROW_TILES))
        last_o_banks = [psum_tu.tile([P, L], F32, name="last_o_bank", tag="bank") for m in range(ROW_TILES)]
        stage_two(last, [bank[:] for bank in last_o_banks])
        for m in range(ROW_TILES):
            result = result_pool.tile([P, L], F32, name="last_result", tag="last_result")
            add_affine(result[:], last, m, last_o_banks[m][:])
            nc.sync.dma_start(out=out[last, m * P : (m + 1) * P, :, 0], in_=result[:])
